import numpy as np
import ml_dtypes


def mxq(x, axis, fmt="e4m3"):
    dtype, down = {"e4m3": (ml_dtypes.float8_e4m3fn, 7), "e5m2": (ml_dtypes.float8_e5m2, 14)}[fmt]
    v = np.moveaxis(np.asarray(x, np.float32).astype(ml_dtypes.bfloat16).astype(np.float64), axis, -1)
    blocks = v.reshape(v.shape[:-1] + (-1, 32))
    amax = np.abs(blocks).max(-1, keepdims=True)
    byte = np.maximum(np.where(amax > 0, np.frexp(amax)[1] - 1 + 127, 0) - down, 1)
    scale = np.exp2(byte - 127.0)
    codes = (blocks / scale).astype(np.float32).astype(dtype).astype(np.float64)
    return np.moveaxis((codes * scale).reshape(v.shape), -1, axis)


WIDE = False


def mx_kscale(k):
    if not WIDE:
        return np.ones(k)
    levels = np.array([18, -18])
    if k % 512:
        return np.exp2(np.random.permutation(np.resize(levels, k // 32))).repeat(32)
    a = np.empty((k // 512, 16))
    for p in range(k // 512):
        a[p, :8] = np.random.permutation(np.resize(levels, 8))
        for g in range(8):
            far = levels[np.abs(levels - a[p, g]) >= 10]
            a[p, g + 8] = far[np.random.randint(len(far))]
    return np.exp2(a.ravel()).repeat(32)


BF16 = ml_dtypes.bfloat16


def bf(x):
    return np.asarray(x, np.float32).astype(BF16)


def f64(x):
    return np.asarray(x).astype(np.float64)


B, T, P, F, G, R, C, O = 256, 8, 1024, 512, 512, 128, 4, 10
N = B * T


def setup_inputs():
    s = np.repeat(mx_kscale(N)[::T], T)[:, None]
    u = mx_kscale(F)
    v = mx_kscale(G)
    r0 = np.concatenate([np.full(P + F, 1.0 / np.sqrt(P + F)), [0.1]])[:, None]
    r1 = np.concatenate([np.full(G, 1.5 / np.sqrt(G)), [0.1]])[:, None]
    p0 = bf(np.random.standard_normal((N, P)))
    x0 = bf(np.maximum(np.random.standard_normal((N, F)), 0.0) * 0.9)
    col0 = bf(np.array([float(np.random.randint(1, C))]))
    w0_0 = bf(np.random.standard_normal((P + F + 1, G)) * r0)
    b0 = bf(np.random.standard_normal(G) * 0.2)
    w1_0 = bf(np.random.standard_normal((G + 1, F)) * r1)
    b1 = bf(np.random.standard_normal(F) * 0.2)
    c, w0, w1 = f64(col0), f64(w0_0), f64(w1_0)
    a = np.concatenate([f64(p0), f64(x0)], axis=1) @ w0[:P + F] + c * w0[P + F] + f64(b0)
    h = np.roll(np.maximum(a, 0.0).reshape(B, T * G), -R, axis=1).reshape(N, G)
    y = h @ w1[:G] + c * w1[G] + f64(b1)
    gy = np.random.standard_normal((N, F)) * 2.0 * np.exp2(np.random.randint(-6, 1, (N, 1))) / s * u
    return {"primary_input": bf(f64(p0) * s).reshape(B, T * P),
            "prev": bf(f64(x0) * s).reshape(B, T * F),
            "col": bf(f64(col0) * s.min()),
            "W0": bf(w0 / v),
            "b0": b0,
            "W1": bf(w1 * np.concatenate([np.roll(v, -R), [1.0]])[:, None] / u),
            "b1": b1,
            "a": np.asarray(a.reshape(B, T, G), np.float32),
            "y": np.asarray(y.reshape(B, T, F), np.float32),
            "grad_out": bf(np.roll(gy.reshape(B, T * F), R, axis=1))}


def reference(primary_input, prev, col, W0, b0, W1, b1, a, y, grad_out):
    w0, w1, c = f64(W0), f64(W1), f64(col)
    inp = np.concatenate([f64(primary_input).reshape(N, P), f64(prev).reshape(N, F)], axis=1)
    dy = np.roll(f64(grad_out), -R, axis=1).reshape(N, F) * (f64(y).reshape(N, F) > 0.0)
    dh = mxq(dy, 1, "e5m2") @ mxq(w1[:G], 1, "e4m3").T
    da = np.roll(dh.reshape(B, T * G), R, axis=1).reshape(N, G) * (f64(a).reshape(N, G) > 0.0)
    dp = mxq(da, 1, "e5m2") @ mxq(w0[:P], 1, "e4m3").T
    dw = mxq(inp, 0, "e4m3").T @ mxq(da, 0, "e5m2")
    last = c * da.sum(axis=0)
    return dp.reshape(B, T * P), np.concatenate([dw, last[None, :]], axis=0)

@@ -1,0 +1,409 @@
+from contextlib import ExitStack
+
+import concourse.mybir as mybir
+from concourse.masks import make_identity
+
+B, T, P_IN, F, G = 256, 8, 1024, 512, 512
+N = B * T
+C_OUT = P_IN + F
+FLOPS = 2 * N * F * G + 2 * N * G * P_IN + 2 * N * C_OUT * G
+BYTES = 2 * (N * P_IN + N * F + 1 + P_IN * G + G * F + N * F) + 4 * (N * G + N * F) + 4 * (N * P_IN + (C_OUT + 1) * G)
+
+F32 = mybir.dt.float32
+BF16 = mybir.dt.bfloat16
+U32 = mybir.dt.uint32
+U8 = mybir.dt.uint8
+E4 = mybir.dt.float8_e4m3fn_x4
+E5 = mybir.dt.float8_e5m2_x4
+ALU = mybir.AluOpType
+
+PART = 128
+PACK = 4
+GROUP = PART * PACK
+GROUPS = N // GROUP
+ROLL = 128
+
+
+def tile_capsuleneuralnetwork_pa_v_kernel(
+    tc, primary_input, prev, col, W0, b0, W1, b1, a, y, grad_out, out_0, out_1
+):
+    nc = tc.nc
+
+    p_dram = primary_input.rearrange("b (t w) -> (b t) w", t=T).rearrange("(g p j) w -> g p j w", p=PART, j=PACK)
+    x_dram = prev.rearrange("b (t w) -> (b t) w", t=T).rearrange("(g p j) w -> g p j w", p=PART, j=PACK)
+    a_dram = a.rearrange("b t w -> (b t) w").rearrange("(g p j) w -> g p j w", p=PART, j=PACK)
+    y_dram = y.rearrange("b t w -> (b t) w").rearrange("(g p j) w -> g p j w", p=PART, j=PACK)
+    o_dram = out_0.rearrange("b (t w) -> (b t) w", t=T).rearrange("(g p j) w -> g p j w", p=PART, j=PACK)
+    gr_rows = grad_out.rearrange("b (h w) -> (b h) w", h=2)
+    gr_half = grad_out.rearrange("(g b) (h w) -> h b g w", b=PART // 2, h=2)
+
+    with ExitStack() as ctx:
+        pool = ctx.enter_context(tc.tile_pool(name="pool", bufs=1))
+        psum = ctx.enter_context(tc.psum_pool(name="psum", bufs=1))
+
+        def bank(tag):
+            return psum.tile([PART, 512], F32, name=tag, tag=tag, bufs={"tp": 2, "dh": 3, "acc": 2, "c": 1}[tag])
+
+        ident = pool.tile([PART, PART], F32, name="ident")
+        swap = pool.tile([PART, PART], F32, name="swap")
+        make_identity(nc, ident[:])
+        for h in range(2):
+            nc.gpsimd.tensor_copy(
+                out=swap[:].rearrange("p (b h) -> p b h", h=2)[:, :, h],
+                in_=ident[:].rearrange("p (b h) -> p b h", h=2)[:, :, 1 - h],
+            )
+        col_b = pool.tile([PART, 1], BF16, name="col_b")
+        nc.gpsimd.dma_start(out=col_b[:], in_=col.partition_broadcast(PART))
+
+        q_all = pool.tile([PART, GROUPS, 4 * F], BF16, name="q_all")
+        w1_codes = pool.tile([PART, G], U32, name="w1_codes", align_bytes=64)
+        w1_scales = pool.tile([PART, G], U8, name="w1_scales", align_bytes=64)
+        w0_codes = pool.tile([PART, P_IN], U32, name="w0_codes", align_bytes=64)
+        w0_scales = pool.tile([PART, P_IN], U8, name="w0_scales", align_bytes=64)
+
+        ctx.enter_context(tc.manual_schedule())
+
+        y_t, a_t, p_t, x_t = {}, {}, {}, {}
+
+        def load_y(g):
+            y_t[g] = pool.tile([PART, PACK, F], F32, name="y_sb", tag="y_sb", bufs=2)
+            nc.sync.dma_start(out=y_t[g][:, 0:2, :], in_=y_dram[g][:, 0:2, :])
+            nc.sync.dma_start(out=q_all[:, g, 0 : 4 * F - ROLL], in_=gr_rows[g * PART : (g + 1) * PART, ROLL : 4 * F])
+            if g == 0:
+                for h in range(2):
+                    nc.sync.dma_start(
+                        out=q_all[h:PART:2, :, 4 * F - ROLL : 4 * F], in_=gr_half[1 - h][:, :, 0:ROLL]
+                    )
+            nc.sync.dma_start(out=y_t[g][:, 2:4, :], in_=y_dram[g][:, 2:4, :])
+
+        def load_a(g):
+            a_t[g] = pool.tile([PART, PACK, G], F32, name="a_sb", tag="a_sb", bufs=2)
+            for i in range(2):
+                nc.sync.dma_start(out=a_t[g][:, 2 * i : 2 * i + 2, :], in_=a_dram[g][:, 2 * i : 2 * i + 2, :])
+
+        def load_p(g):
+            p_t[g] = pool.tile([PART, PACK, P_IN], BF16, name="p_sb", tag="p_sb", bufs=3)
+            nc.sync.dma_start(out=p_t[g][:], in_=p_dram[g])
+
+        def load_x(g):
+            x_t[g] = pool.tile([PART, PACK, F], BF16, name="x_sb", tag="x_sb", bufs=3)
+            nc.sync.dma_start(out=x_t[g][:], in_=x_dram[g])
+
+        def transpose_pair(words, grouped, first, engine):
+            tp = bank("tp")
+            for i in range(2):
+                for u in range(2):
+                    nc.tensor.transpose(tp[:, (2 * i + u) * 128 : (2 * i + u + 1) * 128], words[i][:, u:256:2], ident[:])
+            dst = grouped.rearrange("p n k -> p (n k)").bitcast(F32)[:, 2 * first : 2 * first + 512]
+            engine(
+                out=dst.rearrange("p (t r u) -> p t r u", t=2, u=2),
+                in_=tp[:].rearrange("p (t u r) -> p t r u", t=2, u=2),
+            )
+
+        w1_raw = pool.tile([PART, PACK, F], BF16, name="w1_raw", tag="x_sb", bufs=3)
+        nc.sync.dma_start(out=w1_raw[:], in_=W1[0:G, :].rearrange("(m t) k -> m t k", t=PACK))
+        load_y(0)
+        load_a(0)
+        w0_raw = pool.tile([PART, 2, PACK, G], BF16, name="w0_raw", tag="p_sb", bufs=3)
+        nc.sync.dma_start(out=w0_raw[:], in_=W0[0:P_IN, :].rearrange("(n m t) k -> m n t k", n=2, t=PACK))
+        load_p(0)
+        load_y(1)
+        load_x(0)
+        load_a(1)
+        load_p(1)
+        load_x(1)
+
+        def stage_tile():
+            return pool.tile([PART, 512, PACK], BF16, name="stage", tag="stage", bufs=3, align_bytes=64)
+
+        w1_g = stage_tile()
+        w1_words = w1_raw[:].rearrange("p t k -> p (t k)").bitcast(F32)
+        for s in range(2):
+            transpose_pair(
+                [w1_words[:, 256 * (2 * s + i) : 256 * (2 * s + i + 1)] for i in range(2)],
+                w1_g[:], 256 * s, nc.scalar.copy if s == 0 else nc.vector.tensor_copy,
+            )
+        nc.vector.quantize_mx(out=w1_codes[:].bitcast(E4), scales=w1_scales[:], in_=w1_g[:].rearrange("p n k -> p (n k)"))
+
+        ic, isc, staged = {}, {}, {}
+
+        def interleave(k):
+            g, c = divmod(k, 3)
+            src = x_t[g][:] if c == 2 else p_t[g][:, :, 512 * c : 512 * (c + 1)]
+            staged[k] = stage_tile()
+            copy = nc.scalar.copy if c == 2 else nc.vector.tensor_copy
+            copy(
+                out=staged[k][:].rearrange("p (c i) t -> p c t i", i=4),
+                in_=src.rearrange("p t (c i) -> p c t i", i=4),
+            )
+
+        def quantize_chunk(k):
+            g, c = divmod(k, 3)
+            if g not in ic:
+                ic[g] = pool.tile([PART, C_OUT], U32, name="ic", tag="ic", bufs=GROUPS, align_bytes=64)
+                isc[g] = pool.tile([PART, C_OUT], U8, name="isc", tag="isc", bufs=GROUPS, align_bytes=64)
+            cols = slice(512 * c, 512 * (c + 1))
+            nc.vector.quantize_mx(
+                out=ic[g][:, cols].bitcast(E4), scales=isc[g][:, cols], in_=staged[k][:].rearrange("p n k -> p (n k)")
+            )
+
+        ac, asc = {}, {}
+        dgc, dgs = {}, {}
+        c_bank = bank("c")
+
+        def dp_tile(g, j, tags=("acc", "acc"), engines=None, store=True):
+            ob = pool.tile([PART, P_IN], F32, name="ob", tag="ob", bufs=5)
+            for n in range(2):
+                acc = bank(tags[n])
+                nc.tensor.matmul_mx(
+                    out=acc[:],
+                    lhsT=dgc[g][:, 128 * j : 128 * (j + 1)].bitcast(E5),
+                    lhsT_scale=dgs[g][:, 128 * j : 128 * (j + 1)],
+                    rhs=w0_codes[:, 512 * n : 512 * (n + 1)].bitcast(E4),
+                    rhs_scale=w0_scales[:, 512 * n : 512 * (n + 1)],
+                    start=True,
+                    stop=True,
+                )
+                copy = engines[n] if engines else nc.scalar.copy
+                copy(
+                    out=ob[:, 512 * n : 512 * (n + 1)].rearrange("p (m t) -> p m t", t=4),
+                    in_=acc[:].rearrange("p (t m) -> p m t", t=4),
+                )
+            nc.sync.dma_start(out=o_dram[g][:, j, :], in_=ob[:])
+
+        dw_bank = {}
+
+        def dw_pass(i, g):
+            nc.tensor.matmul_mx(
+                out=dw_bank[i][:],
+                lhsT=ic[g][:, 128 * i : 128 * (i + 1)].bitcast(E4),
+                lhsT_scale=isc[g][:, 128 * i : 128 * (i + 1)],
+                rhs=ac[g][:].bitcast(E5),
+                rhs_scale=asc[g][:],
+                start=(g == 0),
+                stop=(g == GROUPS - 1),
+            )
+
+        def dw_out(i, copy):
+            wb = pool.tile([PART, G], F32, name="wb", tag="wb", bufs=6)
+            copy(
+                out=wb[:].rearrange("p (m t) -> p m t", t=4),
+                in_=dw_bank[i][:].rearrange("p (t m) -> p m t", t=4),
+            )
+            nc.sync.dma_start(out=out_1[128 * i : 128 * (i + 1), :], in_=wb[:])
+
+        def group_step(g):
+            last = g == GROUPS - 1
+            if g > 0:
+                dp_tile(g - 1, 0)
+            dy = pool.tile([PART, PACK, F], BF16, name="dy", tag="dy", bufs=1)
+            for i in range(2):
+                nc.vector.scalar_tensor_tensor(
+                    out=dy[:, 2 * i : 2 * i + 2, :],
+                    in0=y_t[g][:, 2 * i : 2 * i + 2, :],
+                    scalar=0.0,
+                    in1=q_all[:, g, 1024 * i : 1024 * (i + 1)].rearrange("p (j w) -> p j w", j=2),
+                    op0=ALU.is_gt,
+                    op1=ALU.mult,
+                )
+            if g == 0:
+                load_y(2)
+            dyg = pool.tile([PART, 640, PACK], BF16, name="dyg", tag="dyg", bufs=1, align_bytes=64)
+            dyw = dy[:].rearrange("p j w -> p (j w)").bitcast(F32)
+            for s in range(2):
+                transpose_pair([dyw[:, 256 * (2 * s + i) : 256 * (2 * s + i + 1)] for i in range(2)], dyg[:], 256 * s, nc.scalar.copy)
+            tp = bank("tp")
+            for u in range(2):
+                nc.tensor.transpose(tp[:, 128 * u : 128 * (u + 1)], dyw[:, 768 + u : 1024 : 2], swap[:])
+            nc.scalar.copy(
+                out=dyg[:].rearrange("p n k -> p (n k)").bitcast(F32)[:, 1024:1280].rearrange("p (r u) -> p r u", u=2),
+                in_=tp[:, 0:256].rearrange("p (u r) -> p r u", u=2),
+            )
+            if g == 1:
+                interleave(1)
+            if g == 2:
+                interleave(4)
+                quantize_chunk(2)
+            if g == 3:
+                interleave(7)
+                quantize_chunk(5)
+            if g > 0:
+                dp_tile(g - 1, 1)
+            dyc = pool.tile([PART, 640], U32, name="dyc", tag="dyc", bufs=2, align_bytes=64)
+            dys = pool.tile([PART, 640], U8, name="dys", tag="dys", bufs=2, align_bytes=64)
+            for lo, hi in ((512, 640), (0, 512)):
+                nc.vector.quantize_mx(
+                    out=dyc[:, lo:hi].bitcast(E5), scales=dys[:, lo:hi], in_=dyg[:, lo:hi, :].rearrange("p n k -> p (n k)")
+                )
+            dh = {}
+
+            def dh_mm(s):
+                dh[s] = bank("dh")
+                nc.tensor.matmul_mx(
+                    out=dh[s][:],
+                    lhsT=dyc[:, 128 * s : 128 * (s + 1)].bitcast(E5),
+                    lhsT_scale=dys[:, 128 * s : 128 * (s + 1)],
+                    rhs=w1_codes[:].bitcast(E4),
+                    rhs_scale=w1_scales[:],
+                    start=True,
+                    stop=True,
+                )
+
+            for s in (4, 0, 1):
+                dh_mm(s)
+            if g > 0:
+                dp_tile(g - 1, 2)
+            if g == 1:
+                interleave(3)
+                quantize_chunk(1)
+            if g == 2:
+                interleave(6)
+                quantize_chunk(4)
+            da = pool.tile([PART, PACK, G], F32, name="da", tag="da", bufs=1)
+
+            def mask(j, s, lo, hi, src):
+                nc.vector.scalar_tensor_tensor(
+                    out=da[:, j, :].rearrange("p (t m) -> p t m", t=4)[:, :, lo:hi],
+                    in0=a_t[g][:, j, :].rearrange("p (m t) -> p t m", t=4)[:, :, lo:hi],
+                    scalar=0.0,
+                    in1=dh[s][:].rearrange("p (t m) -> p t m", t=4)[:, :, src : src + hi - lo],
+                    op0=ALU.is_gt,
+                    op1=ALU.mult,
+                )
+
+            mask(0, 4, 0, 32, 96)
+            mask(0, 0, 32, 128, 0)
+            dh_mm(2)
+            mask(1, 0, 0, 32, 96)
+            mask(1, 1, 32, 128, 0)
+            dh_mm(3)
+            mask(2, 1, 0, 32, 96)
+            mask(2, 2, 32, 128, 0)
+            mask(3, 2, 0, 32, 96)
+            mask(3, 3, 32, 128, 0)
+            if g == 0:
+                load_a(2)
+            if g > 0:
+                dp_tile(g - 1, 3)
+            if last:
+                for i in range(2):
+                    dw_bank[i] = bank("acc")
+                    for gg in range(3):
+                        dw_pass(i, gg)
+            dag = pool.tile([PART, GROUP, PACK], BF16, name="dag", tag="dag", bufs=1, align_bytes=64)
+            for j in range(PACK):
+                tp = bank("tp")
+                for t in range(4):
+                    nc.tensor.transpose(tp[:, 128 * t : 128 * (t + 1)], da[:, j, 128 * t : 128 * (t + 1)], ident[:])
+                for t in range(4):
+                    nc.tensor.matmul(
+                        out=c_bank[:, 128 * t : 128 * (t + 1)],
+                        lhsT=da[:, j, 128 * t : 128 * (t + 1)],
+                        rhs=ident[:],
+                        is_transpose=True,
+                        start=(g == 0 and j == 0 and t == 0),
+                        stop=(last and j == 3 and t == 3),
+                    )
+                nc.scalar.copy(out=dag[:, 128 * j : 128 * (j + 1), :], in_=tp[:].rearrange("p (t n) -> p n t", t=4))
+            at = pool.tile([PART, G, PACK], BF16, name="at", tag="at", bufs=1, align_bytes=64)
+            ac[g] = pool.tile([PART, G], U32, name="ac", tag="ac", bufs=GROUPS, align_bytes=64)
+            asc[g] = pool.tile([PART, G], U8, name="asc", tag="asc", bufs=GROUPS, align_bytes=64)
+            dgc[g] = pool.tile([PART, GROUP], U32, name="dgc", tag="dgc", bufs=2, align_bytes=64)
+            dgs[g] = pool.tile([PART, GROUP], U8, name="dgs", tag="dgs", bufs=2, align_bytes=64)
+            if g == 2:
+                quantize_chunk(6)
+            if g == 3:
+                quantize_chunk(7)
+            nc.vector.tensor_copy(
+                out=at[:].rearrange("p (c i) j -> p c j i", i=4), in_=da[:].rearrange("p j (c i) -> p c j i", i=4)
+            )
+            if g == 0:
+                interleave(0)
+                w0_g = [stage_tile(), stage_tile()]
+                w0_words = w0_raw[:].rearrange("p n t k -> p (n t k)").bitcast(F32)
+                for s in range(4):
+                    transpose_pair(
+                        [w0_words[:, 256 * (2 * s + i) : 256 * (2 * s + i + 1)] for i in range(2)],
+                        w0_g[s // 2][:], 256 * (s % 2), nc.scalar.copy,
+                    )
+            if g == 1:
+                quantize_chunk(3)
+            if g == 3:
+                interleave(9)
+            nc.vector.quantize_mx(out=ac[g][:].bitcast(E5), scales=asc[g][:], in_=at[:].rearrange("p n k -> p (n k)"))
+            if g == 0:
+                quantize_chunk(0)
+                for n in range(2):
+                    nc.vector.quantize_mx(
+                        out=w0_codes[:, 512 * n : 512 * (n + 1)].bitcast(E4),
+                        scales=w0_scales[:, 512 * n : 512 * (n + 1)],
+                        in_=w0_g[n][:].rearrange("p n k -> p (n k)"),
+                    )
+            if g == 3:
+                quantize_chunk(9)
+            nc.vector.quantize_mx(out=dgc[g][:].bitcast(E5), scales=dgs[g][:], in_=dag[:].rearrange("p n k -> p (n k)"))
+            if g > 0:
+                interleave(3 * (g - 1) + 2)
+            if g == 1:
+                load_p(2)
+                load_x(2)
+                load_y(3)
+                load_a(3)
+            if g == 2:
+                load_p(3)
+                load_x(3)
+
+        for g in range(GROUPS):
+            group_step(g)
+
+        seq = ["acc", "acc", "dh", "dh", "dh", "tp", "tp"]
+        for i in range(2, 7):
+            dw_bank[i] = bank(seq[i])
+            for gg in range(3):
+                dw_pass(i, gg)
+        for i in range(4):
+            dw_pass(i, 3)
+        interleave(10)
+        quantize_chunk(8)
+        interleave(11)
+        red = pool.tile([PART, 4], F32, name="red")
+        red_col = pool.tile([PART, 4], F32, name="red_col")
+        nc.vector.tensor_reduce(
+            out=red[:], in_=c_bank[:].rearrange("p (t n) -> p t n", t=4), axis=mybir.AxisListType.X, op=ALU.add
+        )
+        quantize_chunk(10)
+        nc.vector.tensor_scalar(out=red_col[:], in0=red[:], scalar1=col_b[:, 0:1], scalar2=None, op0=ALU.mult)
+        for i in range(4):
+            dw_out(i, nc.scalar.copy if i % 2 == 0 else nc.vector.tensor_copy)
+        for i in range(4, 7):
+            dw_pass(i, 3)
+        quantize_chunk(11)
+        for i in range(4, 7):
+            dw_out(i, nc.scalar.copy if i % 2 == 0 else nc.vector.tensor_copy)
+        last_bank = bank("c")
+        for t in range(4):
+            nc.tensor.matmul(
+                out=last_bank[:, 128 * t : 128 * (t + 1)],
+                lhsT=red_col[:, t : t + 1].to_broadcast([PART, PART]),
+                rhs=ident[:],
+                start=True,
+                stop=True,
+            )
+        row = pool.tile([1, G], F32, name="row")
+        nc.vector.tensor_copy(
+            out=row[:].rearrange("p (m t) -> p m t", t=4), in_=last_bank[0:1, :].rearrange("p (t m) -> p m t", t=4)
+        )
+        nc.sync.dma_start(out=out_1[C_OUT : C_OUT + 1, :], in_=row[:])
+        n_bank = 0
+        for item in ("dp0", "dw7", "dp1", "dw8", "dp2", "dw9", "dp3", "dw10", "dw11"):
+            index = int(item[2:])
+            if item.startswith("dp"):
+                tags = (seq[n_bank % 7], seq[(n_bank + 1) % 7])
+                n_bank += 2
+                dp_tile(3, index, tags, (nc.scalar.copy, nc.vector.tensor_copy))
+            else:
+                dw_bank[index] = bank(seq[n_bank % 7])
+                n_bank += 1
+                for gg in range(GROUPS):
+                    dw_pass(index, gg)
+                dw_out(index, nc.scalar.copy if index % 2 == 0 else nc.vector.tensor_copy)

@@ -67,22 +67,17 @@ def tile_capsuleneuralnetwork_pa_v_kernel(
 
         def load_y(g):
             y_t[g] = pool.tile([PART, PACK, F], F32, name="y_sb", tag="y_sb", bufs=2)
-            nc.sync.dma_start(out=y_t[g][:, 0:2, :], in_=y_dram[g][:, 0:2, :])
+            pieces = ((0, 2), (2, 4)) if g == 0 else ((0, 4),)
             nc.sync.dma_start(out=q_all[:, g, 0 : 4 * F - ROLL], in_=gr_rows[g * PART : (g + 1) * PART, ROLL : 4 * F])
-            if g == 0:
-                for h in range(2):
-                    nc.sync.dma_start(
-                        out=q_all[h:PART:2, :, 4 * F - ROLL : 4 * F], in_=gr_half[1 - h][:, :, 0:ROLL]
-                    )
-            nc.sync.dma_start(out=y_t[g][:, 2:4, :], in_=y_dram[g][:, 2:4, :])
+            for lo, hi in pieces:
+                nc.sync.dma_start(out=y_t[g][:, lo:hi, :], in_=y_dram[g][:, lo:hi, :])
 
         def load_a(g):
             a_t[g] = pool.tile([PART, PACK, G], F32, name="a_sb", tag="a_sb", bufs=2)
-            for i in range(2):
-                nc.sync.dma_start(out=a_t[g][:, 2 * i : 2 * i + 2, :], in_=a_dram[g][:, 2 * i : 2 * i + 2, :])
+            nc.sync.dma_start(out=a_t[g][:], in_=a_dram[g])
 
         def load_p(g):
-            p_t[g] = pool.tile([PART, PACK, P_IN], BF16, name="p_sb", tag="p_sb", bufs=3)
+            p_t[g] = pool.tile([PART, PACK, P_IN], BF16, name="p_sb", tag="p_sb", bufs=4)
             nc.sync.dma_start(out=p_t[g][:], in_=p_dram[g])
 
         def load_x(g):
@@ -100,61 +95,51 @@ def tile_capsuleneuralnetwork_pa_v_kernel(
                 in_=tp[:].rearrange("p (t u r) -> p t r u", t=2, u=2),
             )
 
+        for h in range(2):
+            nc.scalar.dma_start(out=q_all[h:PART:2, :, 4 * F - ROLL : 4 * F], in_=gr_half[1 - h][:, :, 0:ROLL])
         w1_raw = pool.tile([PART, PACK, F], BF16, name="w1_raw", tag="x_sb", bufs=3)
         nc.sync.dma_start(out=w1_raw[:], in_=W1[0:G, :].rearrange("(m t) k -> m t k", t=PACK))
         load_y(0)
         load_a(0)
-        w0_raw = pool.tile([PART, 2, PACK, G], BF16, name="w0_raw", tag="p_sb", bufs=3)
-        nc.sync.dma_start(out=w0_raw[:], in_=W0[0:P_IN, :].rearrange("(n m t) k -> m n t k", n=2, t=PACK))
-        load_p(0)
-        load_y(1)
         load_x(0)
+        load_y(1)
+        w0_raw = pool.tile([PART, 2, PACK, G], BF16, name="w0_raw", tag="p_sb", bufs=4)
+        nc.sync.dma_start(out=w0_raw[:], in_=W0[0:P_IN, :].rearrange("(n m t) k -> m n t k", n=2, t=PACK))
         load_a(1)
-        load_p(1)
         load_x(1)
 
         def stage_tile():
             return pool.tile([PART, 512, PACK], BF16, name="stage", tag="stage", bufs=3, align_bytes=64)
 
-        w1_g = stage_tile()
-        w1_words = w1_raw[:].rearrange("p t k -> p (t k)").bitcast(F32)
-        for s in range(2):
-            transpose_pair(
-                [w1_words[:, 256 * (2 * s + i) : 256 * (2 * s + i + 1)] for i in range(2)],
-                w1_g[:], 256 * s, nc.scalar.copy if s == 0 else nc.vector.tensor_copy,
-            )
-        nc.vector.quantize_mx(out=w1_codes[:].bitcast(E4), scales=w1_scales[:], in_=w1_g[:].rearrange("p n k -> p (n k)"))
-
         ic, isc, staged = {}, {}, {}
 
-        def interleave(k):
-            g, c = divmod(k, 3)
+        def interleave(g, c, copy):
             src = x_t[g][:] if c == 2 else p_t[g][:, :, 512 * c : 512 * (c + 1)]
-            staged[k] = stage_tile()
-            copy = nc.scalar.copy if c == 2 else nc.vector.tensor_copy
+            staged[g, c] = stage_tile()
             copy(
-                out=staged[k][:].rearrange("p (c i) t -> p c t i", i=4),
+                out=staged[g, c][:].rearrange("p (c i) t -> p c t i", i=4),
                 in_=src.rearrange("p t (c i) -> p c t i", i=4),
             )
 
-        def quantize_chunk(k):
-            g, c = divmod(k, 3)
-            if g not in ic:
-                ic[g] = pool.tile([PART, C_OUT], U32, name="ic", tag="ic", bufs=GROUPS, align_bytes=64)
-                isc[g] = pool.tile([PART, C_OUT], U8, name="isc", tag="isc", bufs=GROUPS, align_bytes=64)
-            cols = slice(512 * c, 512 * (c + 1))
+        def quantize_chunk(g, c):
+            ic[g, c] = pool.tile([PART, 512], U32, name="ic", tag="ic", bufs=12, align_bytes=64)
+            isc[g, c] = pool.tile([PART, 512], U8, name="isc", tag="isc", bufs=12, align_bytes=64)
             nc.vector.quantize_mx(
-                out=ic[g][:, cols].bitcast(E4), scales=isc[g][:, cols], in_=staged[k][:].rearrange("p n k -> p (n k)")
+                out=ic[g, c][:].bitcast(E4), scales=isc[g, c][:], in_=staged[g, c][:].rearrange("p n k -> p (n k)")
             )
 
-        ac, asc = {}, {}
-        dgc, dgs = {}, {}
+        vcopy, scopy = nc.vector.tensor_copy, nc.scalar.copy
+        ac, asc, dgc, dgs, dyg, dyc, dys, dh, da, dag = ({} for i in range(10))
         c_bank = bank("c")
 
-        def dp_tile(g, j, tags=("acc", "acc"), engines=None, store=True):
-            ob = pool.tile([PART, P_IN], F32, name="ob", tag="ob", bufs=5)
+        ob_t = {}
+
+        def dp_tile(g, j, engines):
+            if j % 2 == 0:
+                ob_t[0] = pool.tile([PART, 2, P_IN], F32, name="ob", tag="ob", bufs=4)
+            ob = ob_t[0][:, j % 2, :]
             for n in range(2):
-                acc = bank(tags[n])
+                acc = bank("acc")
                 nc.tensor.matmul_mx(
                     out=acc[:],
                     lhsT=dgc[g][:, 128 * j : 128 * (j + 1)].bitcast(E5),
@@ -164,20 +149,198 @@ def tile_capsuleneuralnetwork_pa_v_kernel(
                     start=True,
                     stop=True,
                 )
-                copy = engines[n] if engines else nc.scalar.copy
-                copy(
+                engines[n](
                     out=ob[:, 512 * n : 512 * (n + 1)].rearrange("p (m t) -> p m t", t=4),
                     in_=acc[:].rearrange("p (t m) -> p m t", t=4),
                 )
-            nc.sync.dma_start(out=o_dram[g][:, j, :], in_=ob[:])
+            if j % 2:
+                nc.sync.dma_start(out=o_dram[g][:, j - 1 : j + 1, :], in_=ob_t[0][:])
 
+        def dy_half(g, i):
+            if i == 0:
+                dyg[g, 0] = pool.tile([PART, PACK, F], BF16, name="dy", tag="dy", bufs=1)
+            nc.vector.scalar_tensor_tensor(
+                out=dyg[g, 0][:, 2 * i : 2 * i + 2, :],
+                in0=y_t[g][:, 2 * i : 2 * i + 2, :],
+                scalar=0.0,
+                in1=q_all[:, g, 1024 * i : 1024 * (i + 1)].rearrange("p (j w) -> p j w", j=2),
+                op0=ALU.is_gt,
+                op1=ALU.mult,
+            )
+
+        def dy_transposes(g):
+            dyg[g, 1] = pool.tile([PART, 640, PACK], BF16, name="dyg", tag="dyg", bufs=1, align_bytes=64)
+            dyw = dyg[g, 0][:].rearrange("p j w -> p (j w)").bitcast(F32)
+            for s in range(2):
+                transpose_pair(
+                    [dyw[:, 256 * (2 * s + i) : 256 * (2 * s + i + 1)] for i in range(2)], dyg[g, 1][:], 256 * s, scopy
+                )
+            tp = bank("tp")
+            for u in range(2):
+                nc.tensor.transpose(tp[:, 128 * u : 128 * (u + 1)], dyw[:, 768 + u : 1024 : 2], swap[:])
+            scopy(
+                out=dyg[g, 1][:].rearrange("p n k -> p (n k)").bitcast(F32)[:, 1024:1280].rearrange("p (r u) -> p r u", u=2),
+                in_=tp[:, 0:256].rearrange("p (u r) -> p r u", u=2),
+            )
+
+        def dy_quantize(g):
+            dyc[g] = pool.tile([PART, 640], U32, name="dyc", tag="dyc", bufs=2, align_bytes=64)
+            dys[g] = pool.tile([PART, 640], U8, name="dys", tag="dys", bufs=2, align_bytes=64)
+            for lo, hi in ((0, 512), (512, 640)):
+                nc.vector.quantize_mx(
+                    out=dyc[g][:, lo:hi].bitcast(E5),
+                    scales=dys[g][:, lo:hi],
+                    in_=dyg[g, 1][:, lo:hi, :].rearrange("p n k -> p (n k)"),
+                )
+
+        def dh_tile(g, s):
+            dh[g, s] = bank("dh")
+            nc.tensor.matmul_mx(
+                out=dh[g, s][:],
+                lhsT=dyc[g][:, 128 * s : 128 * (s + 1)].bitcast(E5),
+                lhsT_scale=dys[g][:, 128 * s : 128 * (s + 1)],
+                rhs=w1_codes[:].bitcast(E4),
+                rhs_scale=w1_scales[:],
+                start=True,
+                stop=True,
+            )
+
+        def mask(g, j, s, lo, hi, src):
+            nc.vector.scalar_tensor_tensor(
+                out=da[g][:, j, :].rearrange("p (t m) -> p t m", t=4)[:, :, lo:hi],
+                in0=a_t[g][:, j, :].rearrange("p (m t) -> p t m", t=4)[:, :, lo:hi],
+                scalar=0.0,
+                in1=dh[g, s][:].rearrange("p (t m) -> p t m", t=4)[:, :, src : src + hi - lo],
+                op0=ALU.is_gt,
+                op1=ALU.mult,
+            )
+
+        def da_transposes(g, j):
+            if j == 0:
+                dag[g] = pool.tile([PART, GROUP, PACK], BF16, name="dag", tag="dag", bufs=1, align_bytes=64)
+            tp = bank("tp")
+            for t in range(4):
+                nc.tensor.transpose(tp[:, 128 * t : 128 * (t + 1)], da[g][:, j, 128 * t : 128 * (t + 1)], ident[:])
+            for t in range(4):
+                nc.tensor.matmul(
+                    out=c_bank[:, 128 * t : 128 * (t + 1)],
+                    lhsT=da[g][:, j, 128 * t : 128 * (t + 1)],
+                    rhs=ident[:],
+                    is_transpose=True,
+                    start=(g == 0 and j == 0 and t == 0),
+                    stop=(g == 3 and j == 3 and t == 3),
+                )
+            scopy(out=dag[g][:, 128 * j : 128 * (j + 1), :], in_=tp[:].rearrange("p (t n) -> p n t", t=4))
+
+        w1_g = stage_tile()
+        w1_words = w1_raw[:].rearrange("p t k -> p (t k)").bitcast(F32)
+        for s in range(2):
+            transpose_pair(
+                [w1_words[:, 256 * (2 * s + i) : 256 * (2 * s + i + 1)] for i in range(2)],
+                w1_g[:], 256 * s, vcopy if s == 0 else scopy,
+            )
+        nc.vector.quantize_mx(
+            out=w1_codes[:].bitcast(E4), scales=w1_scales[:], in_=w1_g[:].rearrange("p n k -> p (n k)")
+        )
+        dy_half(0, 0)
+        dy_half(0, 1)
+        dy_transposes(0)
+        load_y(2)
+        interleave(0, 2, scopy)
+        dy_quantize(0)
+        for s in (4, 0, 1):
+            dh_tile(0, s)
+
+        def w0_quantize(n):
+            nc.vector.quantize_mx(
+                out=w0_codes[:, 512 * n : 512 * (n + 1)].bitcast(E4),
+                scales=w0_scales[:, 512 * n : 512 * (n + 1)],
+                in_=w0_g[n][:].rearrange("p n k -> p (n k)"),
+            )
+
+        def dp_index(k):
+            if k >= 0:
+                dp_tile(k // 4, k % 4, (scopy, scopy))
+
+        for g in range(GROUPS):
+            da[g] = pool.tile([PART, PACK, G], F32, name="da", tag="da", bufs=1)
+            mask(g, 0, 4, 0, 32, 96)
+            mask(g, 0, 0, 32, 128, 0)
+            dh_tile(g, 2)
+            mask(g, 1, 0, 0, 32, 96)
+            mask(g, 1, 1, 32, 128, 0)
+            dh_tile(g, 3)
+            mask(g, 2, 1, 0, 32, 96)
+            mask(g, 2, 2, 32, 128, 0)
+            mask(g, 3, 2, 0, 32, 96)
+            mask(g, 3, 3, 32, 128, 0)
+            for j in range(PACK):
+                da_transposes(g, j)
+            if g == 0:
+                load_a(2)
+                load_x(2)
+            if g == 1:
+                load_a(3)
+                load_x(3)
+                load_p(0)
+                w0_quantize(1)
+            dp_index(4 * g - 5)
+            if g < 3:
+                dp_index(4 * g - 4)
+                dy_half(g + 1, 0)
+                dy_half(g + 1, 1)
+                dy_transposes(g + 1)
+                if g == 0:
+                    load_y(3)
+                    w0_g = [stage_tile(), stage_tile()]
+                    w0_words = w0_raw[:].rearrange("p n t k -> p (n t k)").bitcast(F32)
+                    for s in range(4):
+                        transpose_pair(
+                            [w0_words[:, 256 * (2 * s + i) : 256 * (2 * s + i + 1)] for i in range(2)],
+                            w0_g[s // 2][:], 256 * (s % 2), scopy,
+                        )
+                dp_index(4 * g - 3)
+            at = pool.tile([PART, G, PACK], BF16, name="at", tag="at", bufs=1, align_bytes=64)
+            ac[g] = pool.tile([PART, G], U32, name="ac", tag="ac", bufs=GROUPS, align_bytes=64)
+            asc[g] = pool.tile([PART, G], U8, name="asc", tag="asc", bufs=GROUPS, align_bytes=64)
+            dgc[g] = pool.tile([PART, GROUP], U32, name="dgc", tag="dgc", bufs=2, align_bytes=64)
+            dgs[g] = pool.tile([PART, GROUP], U8, name="dgs", tag="dgs", bufs=2, align_bytes=64)
+            vcopy(
+                out=at[:].rearrange("p (c i) j -> p c j i", i=4), in_=da[g][:].rearrange("p j (c i) -> p c j i", i=4)
+            )
+            if g == 3:
+                interleave(0, 0, vcopy)
+            nc.vector.quantize_mx(out=dgc[g][:].bitcast(E5), scales=dgs[g][:], in_=dag[g][:].rearrange("p n k -> p (n k)"))
+            nc.vector.quantize_mx(out=ac[g][:].bitcast(E5), scales=asc[g][:], in_=at[:].rearrange("p n k -> p (n k)"))
+            if g < 3:
+                dy_quantize(g + 1)
+                if g == 0:
+                    quantize_chunk(0, 2)
+                    w0_quantize(0)
+                else:
+                    interleave(g, 2, vcopy)
+                if g == 1:
+                    load_p(1)
+                    load_p(2)
+                    load_p(3)
+                if g == 2:
+                    quantize_chunk(1, 2)
+                for s in (4, 0, 1):
+                    dh_tile(g + 1, s)
+                dp_index(4 * g - 2)
+        quantize_chunk(2, 2)
+
+        seq = ["tp", "dh", "dh", "dh", "tp", "tp", "acc", "acc", "dh", "dh", "dh", "tp"]
         dw_bank = {}
 
         def dw_pass(i, g):
+            c, r = divmod(i, 4)
+            if g == 0:
+                dw_bank[i] = bank(seq[i])
             nc.tensor.matmul_mx(
                 out=dw_bank[i][:],
-                lhsT=ic[g][:, 128 * i : 128 * (i + 1)].bitcast(E4),
-                lhsT_scale=isc[g][:, 128 * i : 128 * (i + 1)],
+                lhsT=ic[g, c][:, 128 * r : 128 * (r + 1)].bitcast(E4),
+                lhsT_scale=isc[g, c][:, 128 * r : 128 * (r + 1)],
                 rhs=ac[g][:].bitcast(E5),
                 rhs_scale=asc[g][:],
                 start=(g == 0),
@@ -185,201 +348,48 @@ def tile_capsuleneuralnetwork_pa_v_kernel(
             )
 
         def dw_out(i, copy):
-            wb = pool.tile([PART, G], F32, name="wb", tag="wb", bufs=6)
-            copy(
-                out=wb[:].rearrange("p (m t) -> p m t", t=4),
-                in_=dw_bank[i][:].rearrange("p (t m) -> p m t", t=4),
-            )
-            nc.sync.dma_start(out=out_1[128 * i : 128 * (i + 1), :], in_=wb[:])
+            if i % 4 == 0:
+                ob_t[1] = pool.tile([PART, 4, G], F32, name="wb", tag="ob", bufs=4)
+            wb = ob_t[1][:, i % 4, :]
+            copy(out=wb.rearrange("p (m t) -> p m t", t=4), in_=dw_bank[i][:].rearrange("p (t m) -> p m t", t=4))
+            nc.sync.dma_start(out=out_1[128 * i : 128 * (i + 1), :], in_=wb)
 
-        def group_step(g):
-            last = g == GROUPS - 1
-            if g > 0:
-                dp_tile(g - 1, 0)
-            dy = pool.tile([PART, PACK, F], BF16, name="dy", tag="dy", bufs=1)
-            for i in range(2):
-                nc.vector.scalar_tensor_tensor(
-                    out=dy[:, 2 * i : 2 * i + 2, :],
-                    in0=y_t[g][:, 2 * i : 2 * i + 2, :],
-                    scalar=0.0,
-                    in1=q_all[:, g, 1024 * i : 1024 * (i + 1)].rearrange("p (j w) -> p j w", j=2),
-                    op0=ALU.is_gt,
-                    op1=ALU.mult,
-                )
-            if g == 0:
-                load_y(2)
-            dyg = pool.tile([PART, 640, PACK], BF16, name="dyg", tag="dyg", bufs=1, align_bytes=64)
-            dyw = dy[:].rearrange("p j w -> p (j w)").bitcast(F32)
-            for s in range(2):
-                transpose_pair([dyw[:, 256 * (2 * s + i) : 256 * (2 * s + i + 1)] for i in range(2)], dyg[:], 256 * s, nc.scalar.copy)
-            tp = bank("tp")
-            for u in range(2):
-                nc.tensor.transpose(tp[:, 128 * u : 128 * (u + 1)], dyw[:, 768 + u : 1024 : 2], swap[:])
-            nc.scalar.copy(
-                out=dyg[:].rearrange("p n k -> p (n k)").bitcast(F32)[:, 1024:1280].rearrange("p (r u) -> p r u", u=2),
-                in_=tp[:, 0:256].rearrange("p (u r) -> p r u", u=2),
-            )
-            if g == 1:
-                interleave(1)
-            if g == 2:
-                interleave(4)
-                quantize_chunk(2)
-            if g == 3:
-                interleave(7)
-                quantize_chunk(5)
-            if g > 0:
-                dp_tile(g - 1, 1)
-            dyc = pool.tile([PART, 640], U32, name="dyc", tag="dyc", bufs=2, align_bytes=64)
-            dys = pool.tile([PART, 640], U8, name="dys", tag="dys", bufs=2, align_bytes=64)
-            for lo, hi in ((512, 640), (0, 512)):
-                nc.vector.quantize_mx(
-                    out=dyc[:, lo:hi].bitcast(E5), scales=dys[:, lo:hi], in_=dyg[:, lo:hi, :].rearrange("p n k -> p (n k)")
-                )
-            dh = {}
-
-            def dh_mm(s):
-                dh[s] = bank("dh")
-                nc.tensor.matmul_mx(
-                    out=dh[s][:],
-                    lhsT=dyc[:, 128 * s : 128 * (s + 1)].bitcast(E5),
-                    lhsT_scale=dys[:, 128 * s : 128 * (s + 1)],
-                    rhs=w1_codes[:].bitcast(E4),
-                    rhs_scale=w1_scales[:],
-                    start=True,
-                    stop=True,
-                )
-
-            for s in (4, 0, 1):
-                dh_mm(s)
-            if g > 0:
-                dp_tile(g - 1, 2)
-            if g == 1:
-                interleave(3)
-                quantize_chunk(1)
-            if g == 2:
-                interleave(6)
-                quantize_chunk(4)
-            da = pool.tile([PART, PACK, G], F32, name="da", tag="da", bufs=1)
-
-            def mask(j, s, lo, hi, src):
-                nc.vector.scalar_tensor_tensor(
-                    out=da[:, j, :].rearrange("p (t m) -> p t m", t=4)[:, :, lo:hi],
-                    in0=a_t[g][:, j, :].rearrange("p (m t) -> p t m", t=4)[:, :, lo:hi],
-                    scalar=0.0,
-                    in1=dh[s][:].rearrange("p (t m) -> p t m", t=4)[:, :, src : src + hi - lo],
-                    op0=ALU.is_gt,
-                    op1=ALU.mult,
-                )
-
-            mask(0, 4, 0, 32, 96)
-            mask(0, 0, 32, 128, 0)
-            dh_mm(2)
-            mask(1, 0, 0, 32, 96)
-            mask(1, 1, 32, 128, 0)
-            dh_mm(3)
-            mask(2, 1, 0, 32, 96)
-            mask(2, 2, 32, 128, 0)
-            mask(3, 2, 0, 32, 96)
-            mask(3, 3, 32, 128, 0)
-            if g == 0:
-                load_a(2)
-            if g > 0:
-                dp_tile(g - 1, 3)
-            if last:
-                for i in range(2):
-                    dw_bank[i] = bank("acc")
-                    for gg in range(3):
-                        dw_pass(i, gg)
-            dag = pool.tile([PART, GROUP, PACK], BF16, name="dag", tag="dag", bufs=1, align_bytes=64)
-            for j in range(PACK):
-                tp = bank("tp")
-                for t in range(4):
-                    nc.tensor.transpose(tp[:, 128 * t : 128 * (t + 1)], da[:, j, 128 * t : 128 * (t + 1)], ident[:])
-                for t in range(4):
-                    nc.tensor.matmul(
-                        out=c_bank[:, 128 * t : 128 * (t + 1)],
-                        lhsT=da[:, j, 128 * t : 128 * (t + 1)],
-                        rhs=ident[:],
-                        is_transpose=True,
-                        start=(g == 0 and j == 0 and t == 0),
-                        stop=(last and j == 3 and t == 3),
-                    )
-                nc.scalar.copy(out=dag[:, 128 * j : 128 * (j + 1), :], in_=tp[:].rearrange("p (t n) -> p n t", t=4))
-            at = pool.tile([PART, G, PACK], BF16, name="at", tag="at", bufs=1, align_bytes=64)
-            ac[g] = pool.tile([PART, G], U32, name="ac", tag="ac", bufs=GROUPS, align_bytes=64)
-            asc[g] = pool.tile([PART, G], U8, name="asc", tag="asc", bufs=GROUPS, align_bytes=64)
-            dgc[g] = pool.tile([PART, GROUP], U32, name="dgc", tag="dgc", bufs=2, align_bytes=64)
-            dgs[g] = pool.tile([PART, GROUP], U8, name="dgs", tag="dgs", bufs=2, align_bytes=64)
-            if g == 2:
-                quantize_chunk(6)
-            if g == 3:
-                quantize_chunk(7)
-            nc.vector.tensor_copy(
-                out=at[:].rearrange("p (c i) j -> p c j i", i=4), in_=da[:].rearrange("p j (c i) -> p c j i", i=4)
-            )
-            if g == 0:
-                interleave(0)
-                w0_g = [stage_tile(), stage_tile()]
-                w0_words = w0_raw[:].rearrange("p n t k -> p (n t k)").bitcast(F32)
-                for s in range(4):
-                    transpose_pair(
-                        [w0_words[:, 256 * (2 * s + i) : 256 * (2 * s + i + 1)] for i in range(2)],
-                        w0_g[s // 2][:], 256 * (s % 2), nc.scalar.copy,
-                    )
-            if g == 1:
-                quantize_chunk(3)
-            if g == 3:
-                interleave(9)
-            nc.vector.quantize_mx(out=ac[g][:].bitcast(E5), scales=asc[g][:], in_=at[:].rearrange("p n k -> p (n k)"))
-            if g == 0:
-                quantize_chunk(0)
-                for n in range(2):
-                    nc.vector.quantize_mx(
-                        out=w0_codes[:, 512 * n : 512 * (n + 1)].bitcast(E4),
-                        scales=w0_scales[:, 512 * n : 512 * (n + 1)],
-                        in_=w0_g[n][:].rearrange("p n k -> p (n k)"),
-                    )
-            if g == 3:
-                quantize_chunk(9)
-            nc.vector.quantize_mx(out=dgc[g][:].bitcast(E5), scales=dgs[g][:], in_=dag[:].rearrange("p n k -> p (n k)"))
-            if g > 0:
-                interleave(3 * (g - 1) + 2)
-            if g == 1:
-                load_p(2)
-                load_x(2)
-                load_y(3)
-                load_a(3)
-            if g == 2:
-                load_p(3)
-                load_x(3)
-
-        for g in range(GROUPS):
-            group_step(g)
-
-        seq = ["acc", "acc", "dh", "dh", "dh", "tp", "tp"]
-        for i in range(2, 7):
-            dw_bank[i] = bank(seq[i])
-            for gg in range(3):
-                dw_pass(i, gg)
-        for i in range(4):
+        interleave(3, 2, scopy)
+        for i in range(8, 12):
+            for g in range(3):
+                dw_pass(i, g)
+            dp_index(i)
+        interleave(1, 0, vcopy)
+        quantize_chunk(0, 0)
+        quantize_chunk(3, 2)
+        interleave(2, 0, vcopy)
+        for i in range(8, 12):
             dw_pass(i, 3)
-        interleave(10)
-        quantize_chunk(8)
-        interleave(11)
+        quantize_chunk(1, 0)
+        interleave(3, 0, vcopy)
+        quantize_chunk(2, 0)
         red = pool.tile([PART, 4], F32, name="red")
         red_col = pool.tile([PART, 4], F32, name="red_col")
         nc.vector.tensor_reduce(
             out=red[:], in_=c_bank[:].rearrange("p (t n) -> p t n", t=4), axis=mybir.AxisListType.X, op=ALU.add
         )
-        quantize_chunk(10)
+        dp_index(12)
+        dp_index(13)
+        quantize_chunk(3, 0)
+        interleave(0, 1, vcopy)
         nc.vector.tensor_scalar(out=red_col[:], in0=red[:], scalar1=col_b[:, 0:1], scalar2=None, op0=ALU.mult)
+        dw_out(8, vcopy)
+        dw_out(9, vcopy)
+        dw_out(10, scopy)
+        dw_out(11, scopy)
         for i in range(4):
-            dw_out(i, nc.scalar.copy if i % 2 == 0 else nc.vector.tensor_copy)
-        for i in range(4, 7):
-            dw_pass(i, 3)
-        quantize_chunk(11)
-        for i in range(4, 7):
-            dw_out(i, nc.scalar.copy if i % 2 == 0 else nc.vector.tensor_copy)
+            for g in range(4):
+                dw_pass(i, g)
+            if i < 2:
+                dp_index(14 + i)
+        interleave(1, 1, scopy)
+        quantize_chunk(0, 1)
+        interleave(2, 1, vcopy)
         last_bank = bank("c")
         for t in range(4):
             nc.tensor.matmul(
@@ -389,21 +399,19 @@ def tile_capsuleneuralnetwork_pa_v_kernel(
                 start=True,
                 stop=True,
             )
+        interleave(3, 1, vcopy)
+        quantize_chunk(1, 1)
+        quantize_chunk(2, 1)
+        dw_out(0, scopy)
+        dw_out(1, scopy)
         row = pool.tile([1, G], F32, name="row")
-        nc.vector.tensor_copy(
-            out=row[:].rearrange("p (m t) -> p m t", t=4), in_=last_bank[0:1, :].rearrange("p (t m) -> p m t", t=4)
-        )
+        quantize_chunk(3, 1)
+        dw_out(2, vcopy)
+        dw_out(3, scopy)
+        vcopy(out=row[:].rearrange("p (m t) -> p m t", t=4), in_=last_bank[0:1, :].rearrange("p (t m) -> p m t", t=4))
         nc.sync.dma_start(out=out_1[C_OUT : C_OUT + 1, :], in_=row[:])
-        n_bank = 0
-        for item in ("dp0", "dw7", "dp1", "dw8", "dp2", "dw9", "dp3", "dw10", "dw11"):
-            index = int(item[2:])
-            if item.startswith("dp"):
-                tags = (seq[n_bank % 7], seq[(n_bank + 1) % 7])
-                n_bank += 2
-                dp_tile(3, index, tags, (nc.scalar.copy, nc.vector.tensor_copy))
-            else:
-                dw_bank[index] = bank(seq[n_bank % 7])
-                n_bank += 1
-                for gg in range(GROUPS):
-                    dw_pass(index, gg)
-                dw_out(index, nc.scalar.copy if index % 2 == 0 else nc.vector.tensor_copy)
+        for g in range(4):
+            for i in range(4, 8):
+                dw_pass(i, g)
+        for i in range(4, 8):
+            dw_out(i, scopy if i % 2 == 0 else vcopy)

@@ -88,25 +88,25 @@ def tile_capsuleneuralnetwork_pa_v_kernel(
             tp = bank("tp")
             for i in range(2):
                 for u in range(2):
-                    nc.tensor.transpose(tp[:, (2 * i + u) * 128 : (2 * i + u + 1) * 128], words[i][:, u:256:2], ident[:])
+                    nc.tensor.transpose(tp[:, (2 * i + u) * 128 : (2 * i + u + 1) * 128], words(i, u), ident[:])
             dst = grouped.rearrange("p n k -> p (n k)").bitcast(F32)[:, 2 * first : 2 * first + 512]
             engine(
                 out=dst.rearrange("p (t r u) -> p t r u", t=2, u=2),
                 in_=tp[:].rearrange("p (t u r) -> p t r u", t=2, u=2),
             )
 
-        for h in range(2):
-            nc.scalar.dma_start(out=q_all[h:PART:2, :, 4 * F - ROLL : 4 * F], in_=gr_half[1 - h][:, :, 0:ROLL])
+        load_x(0)
         w1_raw = pool.tile([PART, PACK, F], BF16, name="w1_raw", tag="x_sb", bufs=3)
         nc.sync.dma_start(out=w1_raw[:], in_=W1[0:G, :].rearrange("(m t) k -> m t k", t=PACK))
+        for h in range(2):
+            nc.scalar.dma_start(out=q_all[h:PART:2, :, 4 * F - ROLL : 4 * F], in_=gr_half[1 - h][:, :, 0:ROLL])
         load_y(0)
+        load_x(1)
         load_a(0)
-        load_x(0)
-        load_y(1)
         w0_raw = pool.tile([PART, 2, PACK, G], BF16, name="w0_raw", tag="p_sb", bufs=4)
         nc.sync.dma_start(out=w0_raw[:], in_=W0[0:P_IN, :].rearrange("(n m t) k -> m n t k", n=2, t=PACK))
+        load_y(1)
         load_a(1)
-        load_x(1)
 
         def stage_tile():
             return pool.tile([PART, 512, PACK], BF16, name="stage", tag="stage", bufs=3, align_bytes=64)
@@ -156,28 +156,32 @@ def tile_capsuleneuralnetwork_pa_v_kernel(
             if j % 2:
                 nc.sync.dma_start(out=o_dram[g][:, j - 1 : j + 1, :], in_=ob_t[0][:])
 
-        def dy_half(g, i):
-            if i == 0:
-                dyg[g, 0] = pool.tile([PART, PACK, F], BF16, name="dy", tag="dy", bufs=1)
+        def dy_part(g, u, lo, hi):
+            if (g, 0) not in dyg:
+                dyg[g, 0] = pool.tile([PART, 2, PACK * F // 2], BF16, name="dy", tag="dy", bufs=1)
+            y_flat = y_t[g][:].rearrange("p j w -> p (j w)").rearrange("p (n u e) -> p n u e", u=2, e=2)
+            q_flat = q_all[:, g, :].rearrange("p (n u e) -> p n u e", u=2, e=2)
             nc.vector.scalar_tensor_tensor(
-                out=dyg[g, 0][:, 2 * i : 2 * i + 2, :],
-                in0=y_t[g][:, 2 * i : 2 * i + 2, :],
+                out=dyg[g, 0][:, u, 256 * lo : 256 * hi].rearrange("p (n e) -> p n e", e=2),
+                in0=y_flat[:, 128 * lo : 128 * hi, u, :],
                 scalar=0.0,
-                in1=q_all[:, g, 1024 * i : 1024 * (i + 1)].rearrange("p (j w) -> p j w", j=2),
+                in1=q_flat[:, 128 * lo : 128 * hi, u, :],
                 op0=ALU.is_gt,
                 op1=ALU.mult,
             )
 
         def dy_transposes(g):
             dyg[g, 1] = pool.tile([PART, 640, PACK], BF16, name="dyg", tag="dyg", bufs=1, align_bytes=64)
-            dyw = dyg[g, 0][:].rearrange("p j w -> p (j w)").bitcast(F32)
+            dyw = dyg[g, 0][:].rearrange("p u w -> p (u w)").bitcast(F32)
+
+            def words(j, u):
+                return dyw[:, 512 * u + 128 * j : 512 * u + 128 * (j + 1)]
+
             for s in range(2):
-                transpose_pair(
-                    [dyw[:, 256 * (2 * s + i) : 256 * (2 * s + i + 1)] for i in range(2)], dyg[g, 1][:], 256 * s, scopy
-                )
+                transpose_pair(lambda i, u: words(2 * s + i, u), dyg[g, 1][:], 256 * s, scopy)
             tp = bank("tp")
             for u in range(2):
-                nc.tensor.transpose(tp[:, 128 * u : 128 * (u + 1)], dyw[:, 768 + u : 1024 : 2], swap[:])
+                nc.tensor.transpose(tp[:, 128 * u : 128 * (u + 1)], words(3, u), swap[:])
             scopy(
                 out=dyg[g, 1][:].rearrange("p n k -> p (n k)").bitcast(F32)[:, 1024:1280].rearrange("p (r u) -> p r u", u=2),
                 in_=tp[:, 0:256].rearrange("p (u r) -> p r u", u=2),
@@ -232,24 +236,39 @@ def tile_capsuleneuralnetwork_pa_v_kernel(
                 )
             scopy(out=dag[g][:, 128 * j : 128 * (j + 1), :], in_=tp[:].rearrange("p (t n) -> p n t", t=4))
 
+        interleave(0, 2, vcopy)
+        load_x(2)
         w1_g = stage_tile()
         w1_words = w1_raw[:].rearrange("p t k -> p (t k)").bitcast(F32)
         for s in range(2):
             transpose_pair(
-                [w1_words[:, 256 * (2 * s + i) : 256 * (2 * s + i + 1)] for i in range(2)],
-                w1_g[:], 256 * s, vcopy if s == 0 else scopy,
+                lambda i, u: w1_words[:, 256 * (2 * s + i) + u : 256 * (2 * s + i + 1) : 2], w1_g[:], 256 * s, scopy
             )
+        quantize_chunk(0, 2)
         nc.vector.quantize_mx(
             out=w1_codes[:].bitcast(E4), scales=w1_scales[:], in_=w1_g[:].rearrange("p n k -> p (n k)")
         )
-        dy_half(0, 0)
-        dy_half(0, 1)
+        for lo in (0, 2):
+            for u in range(2):
+                dy_part(0, u, lo, lo + 2)
         dy_transposes(0)
         load_y(2)
-        interleave(0, 2, scopy)
+        interleave(1, 2, vcopy)
         dy_quantize(0)
+        quantize_chunk(1, 2)
         for s in (4, 0, 1):
             dh_tile(0, s)
+
+        w0_g = {}
+        w0_words = w0_raw[:].rearrange("p n t k -> p (n t k)").bitcast(F32)
+
+        def w0_transposes(s):
+            if s % 2 == 0:
+                w0_g[s // 2] = stage_tile()
+            transpose_pair(
+                lambda i, u: w0_words[:, 256 * (2 * s + i) + u : 256 * (2 * s + i + 1) : 2],
+                w0_g[s // 2][:], 256 * (s % 2), scopy,
+            )
 
         def w0_quantize(n):
             nc.vector.quantize_mx(
@@ -261,6 +280,23 @@ def tile_capsuleneuralnetwork_pa_v_kernel(
         def dp_index(k):
             if k >= 0:
                 dp_tile(k // 4, k % 4, (scopy, scopy))
+
+        at = {}
+
+        def da_cast(g):
+            at[0] = pool.tile([PART, G, PACK], BF16, name="at", tag="at", bufs=1, align_bytes=64)
+            vcopy(
+                out=at[0][:].rearrange("p (c i) j -> p c j i", i=4),
+                in_=da[g][:].rearrange("p j (c i) -> p c j i", i=4),
+            )
+
+        def da_quantize(g):
+            ac[g] = pool.tile([PART, G], U32, name="ac", tag="ac", bufs=GROUPS, align_bytes=64)
+            asc[g] = pool.tile([PART, G], U8, name="asc", tag="asc", bufs=GROUPS, align_bytes=64)
+            dgc[g] = pool.tile([PART, GROUP], U32, name="dgc", tag="dgc", bufs=2, align_bytes=64)
+            dgs[g] = pool.tile([PART, GROUP], U8, name="dgs", tag="dgs", bufs=2, align_bytes=64)
+            nc.vector.quantize_mx(out=dgc[g][:].bitcast(E5), scales=dgs[g][:], in_=dag[g][:].rearrange("p n k -> p (n k)"))
+            nc.vector.quantize_mx(out=ac[g][:].bitcast(E5), scales=asc[g][:], in_=at[0][:].rearrange("p n k -> p (n k)"))
 
         for g in range(GROUPS):
             da[g] = pool.tile([PART, PACK, G], F32, name="da", tag="da", bufs=1)
@@ -274,61 +310,50 @@ def tile_capsuleneuralnetwork_pa_v_kernel(
             mask(g, 2, 2, 32, 128, 0)
             mask(g, 3, 2, 0, 32, 96)
             mask(g, 3, 3, 32, 128, 0)
-            for j in range(PACK):
-                da_transposes(g, j)
+            da_transposes(g, 0)
+            da_transposes(g, 1)
+            dp_index(4 * g - 2)
+            da_transposes(g, 2)
+            da_transposes(g, 3)
+            dp_index(4 * g - 1)
             if g == 0:
                 load_a(2)
-                load_x(2)
+                load_x(3)
+                for s in range(4):
+                    w0_transposes(s)
+                da_cast(0)
+                da_quantize(0)
             if g == 1:
                 load_a(3)
-                load_x(3)
                 load_p(0)
-                w0_quantize(1)
-            dp_index(4 * g - 5)
+                load_p(1)
+            if g == 2:
+                load_p(2)
+                load_p(3)
             if g < 3:
-                dp_index(4 * g - 4)
-                dy_half(g + 1, 0)
-                dy_half(g + 1, 1)
+                for u in range(2):
+                    dy_part(g + 1, u, 0, PACK)
                 dy_transposes(g + 1)
-                if g == 0:
-                    load_y(3)
-                    w0_g = [stage_tile(), stage_tile()]
-                    w0_words = w0_raw[:].rearrange("p n t k -> p (n t k)").bitcast(F32)
-                    for s in range(4):
-                        transpose_pair(
-                            [w0_words[:, 256 * (2 * s + i) : 256 * (2 * s + i + 1)] for i in range(2)],
-                            w0_g[s // 2][:], 256 * (s % 2), scopy,
-                        )
-                dp_index(4 * g - 3)
-            at = pool.tile([PART, G, PACK], BF16, name="at", tag="at", bufs=1, align_bytes=64)
-            ac[g] = pool.tile([PART, G], U32, name="ac", tag="ac", bufs=GROUPS, align_bytes=64)
-            asc[g] = pool.tile([PART, G], U8, name="asc", tag="asc", bufs=GROUPS, align_bytes=64)
-            dgc[g] = pool.tile([PART, GROUP], U32, name="dgc", tag="dgc", bufs=2, align_bytes=64)
-            dgs[g] = pool.tile([PART, GROUP], U8, name="dgs", tag="dgs", bufs=2, align_bytes=64)
-            vcopy(
-                out=at[:].rearrange("p (c i) j -> p c j i", i=4), in_=da[g][:].rearrange("p j (c i) -> p c j i", i=4)
-            )
-            if g == 3:
-                interleave(0, 0, vcopy)
-            nc.vector.quantize_mx(out=dgc[g][:].bitcast(E5), scales=dgs[g][:], in_=dag[g][:].rearrange("p n k -> p (n k)"))
-            nc.vector.quantize_mx(out=ac[g][:].bitcast(E5), scales=asc[g][:], in_=at[:].rearrange("p n k -> p (n k)"))
-            if g < 3:
-                dy_quantize(g + 1)
-                if g == 0:
-                    quantize_chunk(0, 2)
-                    w0_quantize(0)
-                else:
-                    interleave(g, 2, vcopy)
-                if g == 1:
-                    load_p(1)
-                    load_p(2)
-                    load_p(3)
+            if g == 0:
+                load_y(3)
+                w0_quantize(0)
+                w0_quantize(1)
+            else:
+                da_cast(g)
                 if g == 2:
-                    quantize_chunk(1, 2)
+                    quantize_chunk(2, 2)
+                if g == 3:
+                    quantize_chunk(3, 2)
+                    interleave(0, 0, vcopy)
+                da_quantize(g)
+            if g < 3:
+                dp_index(4 * g)
+                dy_quantize(g + 1)
+                if g > 0:
+                    interleave(g + 1, 2, vcopy)
                 for s in (4, 0, 1):
                     dh_tile(g + 1, s)
-                dp_index(4 * g - 2)
-        quantize_chunk(2, 2)
+                dp_index(4 * g + 1)
 
         seq = ["tp", "dh", "dh", "dh", "tp", "tp", "acc", "acc", "dh", "dh", "dh", "tp"]
         dw_bank = {}
@@ -354,61 +379,54 @@ def tile_capsuleneuralnetwork_pa_v_kernel(
             copy(out=wb.rearrange("p (m t) -> p m t", t=4), in_=dw_bank[i][:].rearrange("p (t m) -> p m t", t=4))
             nc.sync.dma_start(out=out_1[128 * i : 128 * (i + 1), :], in_=wb)
 
-        interleave(3, 2, scopy)
+        interleave(3, 0, scopy)
         for i in range(8, 12):
             for g in range(3):
                 dw_pass(i, g)
-            dp_index(i)
+            if i >= 10:
+                dp_index(i + 2)
         interleave(1, 0, vcopy)
         quantize_chunk(0, 0)
-        quantize_chunk(3, 2)
         interleave(2, 0, vcopy)
         for i in range(8, 12):
             dw_pass(i, 3)
         quantize_chunk(1, 0)
-        interleave(3, 0, vcopy)
+        interleave(0, 1, vcopy)
         quantize_chunk(2, 0)
+        quantize_chunk(3, 0)
+        interleave(1, 1, vcopy)
         red = pool.tile([PART, 4], F32, name="red")
         red_col = pool.tile([PART, 4], F32, name="red_col")
         nc.vector.tensor_reduce(
             out=red[:], in_=c_bank[:].rearrange("p (t n) -> p t n", t=4), axis=mybir.AxisListType.X, op=ALU.add
         )
-        dp_index(12)
-        dp_index(13)
-        quantize_chunk(3, 0)
-        interleave(0, 1, vcopy)
+        quantize_chunk(0, 1)
         nc.vector.tensor_scalar(out=red_col[:], in0=red[:], scalar1=col_b[:, 0:1], scalar2=None, op0=ALU.mult)
-        dw_out(8, vcopy)
-        dw_out(9, vcopy)
-        dw_out(10, scopy)
-        dw_out(11, scopy)
+        dw_out(8, scopy)
+        dw_out(9, scopy)
+        dw_out(10, vcopy)
+        dw_out(11, vcopy)
         for i in range(4):
             for g in range(4):
                 dw_pass(i, g)
             if i < 2:
                 dp_index(14 + i)
-        interleave(1, 1, scopy)
-        quantize_chunk(0, 1)
+        interleave(3, 1, scopy)
+        quantize_chunk(1, 1)
         interleave(2, 1, vcopy)
         last_bank = bank("c")
         for t in range(4):
-            nc.tensor.matmul(
-                out=last_bank[:, 128 * t : 128 * (t + 1)],
-                lhsT=red_col[:, t : t + 1].to_broadcast([PART, PART]),
-                rhs=ident[:],
-                start=True,
-                stop=True,
+            nc.tensor.transpose(
+                last_bank[:, 128 * t : 128 * (t + 1)], red_col[:, t : t + 1].to_broadcast([PART, PART]), ident[:]
             )
-        interleave(3, 1, vcopy)
-        quantize_chunk(1, 1)
+        dw_out(0, vcopy)
         quantize_chunk(2, 1)
-        dw_out(0, scopy)
-        dw_out(1, scopy)
+        dw_out(1, vcopy)
         row = pool.tile([1, G], F32, name="row")
         quantize_chunk(3, 1)
-        dw_out(2, vcopy)
+        dw_out(2, scopy)
         dw_out(3, scopy)
-        vcopy(out=row[:].rearrange("p (m t) -> p m t", t=4), in_=last_bank[0:1, :].rearrange("p (t m) -> p m t", t=4))
+        scopy(out=row[:].rearrange("p (m t) -> p m t", t=4), in_=last_bank[0:1, :].rearrange("p (t m) -> p m t", t=4))
         nc.sync.dma_start(out=out_1[C_OUT : C_OUT + 1, :], in_=row[:])
         for g in range(4):
             for i in range(4, 8):

@@ -22,6 +22,7 @@ PACK = 4
 GROUP = PART * PACK
 GROUPS = N // GROUP
 ROLL = 128
+W = (8, 8, 3, 2, 1, 1, 1, 2)
 
 
 def tile_capsuleneuralnetwork_pa_v_kernel(
@@ -100,8 +101,9 @@ def tile_capsuleneuralnetwork_pa_v_kernel(
         nc.sync.dma_start(out=w1_raw[:], in_=W1[0:G, :].rearrange("(m t) k -> m t k", t=PACK))
         for h in range(2):
             nc.scalar.dma_start(out=q_all[h:PART:2, :, 4 * F - ROLL : 4 * F], in_=gr_half[1 - h][:, :, 0:ROLL])
-        load_y(0)
         load_x(1)
+        load_y(0)
+        load_p(0)
         load_a(0)
         w0_raw = pool.tile([PART, 2, PACK, G], BF16, name="w0_raw", tag="p_sb", bufs=4)
         nc.sync.dma_start(out=w0_raw[:], in_=W0[0:P_IN, :].rearrange("(n m t) k -> m n t k", n=2, t=PACK))
@@ -109,7 +111,7 @@ def tile_capsuleneuralnetwork_pa_v_kernel(
         load_a(1)
 
         def stage_tile():
-            return pool.tile([PART, 512, PACK], BF16, name="stage", tag="stage", bufs=3, align_bytes=64)
+            return pool.tile([PART, 512, PACK], BF16, name="stage", tag="stage", bufs=4, align_bytes=64)
 
         ic, isc, staged = {}, {}, {}
 
@@ -156,29 +158,35 @@ def tile_capsuleneuralnetwork_pa_v_kernel(
             if j % 2:
                 nc.sync.dma_start(out=o_dram[g][:, j - 1 : j + 1, :], in_=ob_t[0][:])
 
-        def dy_part(g, u, lo, hi):
-            if (g, 0) not in dyg:
-                dyg[g, 0] = pool.tile([PART, 2, PACK * F // 2], BF16, name="dy", tag="dy", bufs=1)
-            y_flat = y_t[g][:].rearrange("p j w -> p (j w)").rearrange("p (n u e) -> p n u e", u=2, e=2)
-            q_flat = q_all[:, g, :].rearrange("p (n u e) -> p n u e", u=2, e=2)
+        def warm(n):
+            for k in range(n):
+                spare = bank("acc")
+                nc.tensor.matmul(out=spare[:, 0:PART], lhsT=ident[:], rhs=ident[:], start=True, stop=True)
+
+        def dy_half(g, i):
+            if i == 0:
+                dyg[g, 0] = pool.tile([PART, PACK * F], BF16, name="dy", tag="dy", bufs=1)
+            cols = slice(1024 * i, 1024 * (i + 1))
             nc.vector.scalar_tensor_tensor(
-                out=dyg[g, 0][:, u, 256 * lo : 256 * hi].rearrange("p (n e) -> p n e", e=2),
-                in0=y_flat[:, 128 * lo : 128 * hi, u, :],
+                out=dyg[g, 0][:, cols],
+                in0=y_t[g][:].rearrange("p j w -> p (j w)")[:, cols],
                 scalar=0.0,
-                in1=q_flat[:, 128 * lo : 128 * hi, u, :],
+                in1=q_all[:, g, cols],
                 op0=ALU.is_gt,
                 op1=ALU.mult,
             )
 
         def dy_transposes(g):
             dyg[g, 1] = pool.tile([PART, 640, PACK], BF16, name="dyg", tag="dyg", bufs=1, align_bytes=64)
-            dyw = dyg[g, 0][:].rearrange("p u w -> p (u w)").bitcast(F32)
+            dyw = dyg[g, 0][:].bitcast(F32)
 
             def words(j, u):
-                return dyw[:, 512 * u + 128 * j : 512 * u + 128 * (j + 1)]
+                return dyw[:, 256 * j + u : 256 * (j + 1) : 2]
 
             for s in range(2):
                 transpose_pair(lambda i, u: words(2 * s + i, u), dyg[g, 1][:], 256 * s, scopy)
+                if g == 0 and s == 0:
+                    warm(W[7])
             tp = bank("tp")
             for u in range(2):
                 nc.tensor.transpose(tp[:, 128 * u : 128 * (u + 1)], words(3, u), swap[:])
@@ -239,23 +247,27 @@ def tile_capsuleneuralnetwork_pa_v_kernel(
         interleave(0, 2, vcopy)
         load_x(2)
         w1_g = stage_tile()
+        warm(W[0])
         w1_words = w1_raw[:].rearrange("p t k -> p (t k)").bitcast(F32)
         for s in range(2):
             transpose_pair(
                 lambda i, u: w1_words[:, 256 * (2 * s + i) + u : 256 * (2 * s + i + 1) : 2], w1_g[:], 256 * s, scopy
             )
+        warm(W[1])
         quantize_chunk(0, 2)
         nc.vector.quantize_mx(
             out=w1_codes[:].bitcast(E4), scales=w1_scales[:], in_=w1_g[:].rearrange("p n k -> p (n k)")
         )
-        for lo in (0, 2):
-            for u in range(2):
-                dy_part(0, u, lo, lo + 2)
-        dy_transposes(0)
-        load_y(2)
         interleave(1, 2, vcopy)
-        dy_quantize(0)
+        dy_half(0, 0)
+        dy_half(0, 1)
+        dy_transposes(0)
+        warm(W[2])
+        load_y(2)
         quantize_chunk(1, 2)
+        interleave(0, 0, vcopy)
+        dy_quantize(0)
+        interleave(0, 1, vcopy)
         for s in (4, 0, 1):
             dh_tile(0, s)
 
@@ -312,30 +324,37 @@ def tile_capsuleneuralnetwork_pa_v_kernel(
             mask(g, 3, 3, 32, 128, 0)
             da_transposes(g, 0)
             da_transposes(g, 1)
+            if g == 0:
+                warm(W[3])
             dp_index(4 * g - 2)
             da_transposes(g, 2)
             da_transposes(g, 3)
+            if g == 0:
+                warm(W[4])
             dp_index(4 * g - 1)
             if g == 0:
                 load_a(2)
                 load_x(3)
                 for s in range(4):
                     w0_transposes(s)
+                    warm(W[5])
                 da_cast(0)
+                quantize_chunk(0, 0)
+                quantize_chunk(0, 1)
                 da_quantize(0)
             if g == 1:
                 load_a(3)
-                load_p(0)
                 load_p(1)
             if g == 2:
                 load_p(2)
                 load_p(3)
             if g < 3:
-                for u in range(2):
-                    dy_part(g + 1, u, 0, PACK)
+                dy_half(g + 1, 0)
+                dy_half(g + 1, 1)
                 dy_transposes(g + 1)
             if g == 0:
                 load_y(3)
+                warm(W[6])
                 w0_quantize(0)
                 w0_quantize(1)
             else:
@@ -344,7 +363,7 @@ def tile_capsuleneuralnetwork_pa_v_kernel(
                     quantize_chunk(2, 2)
                 if g == 3:
                     quantize_chunk(3, 2)
-                    interleave(0, 0, vcopy)
+                    interleave(1, 0, vcopy)
                 da_quantize(g)
             if g < 3:
                 dp_index(4 * g)
@@ -383,25 +402,15 @@ def tile_capsuleneuralnetwork_pa_v_kernel(
         for i in range(8, 12):
             for g in range(3):
                 dw_pass(i, g)
-            if i >= 10:
-                dp_index(i + 2)
-        interleave(1, 0, vcopy)
-        quantize_chunk(0, 0)
         interleave(2, 0, vcopy)
+        quantize_chunk(1, 0)
+        dp_index(12)
         for i in range(8, 12):
             dw_pass(i, 3)
-        quantize_chunk(1, 0)
-        interleave(0, 1, vcopy)
+        dp_index(13)
+        interleave(1, 1, vcopy)
         quantize_chunk(2, 0)
         quantize_chunk(3, 0)
-        interleave(1, 1, vcopy)
-        red = pool.tile([PART, 4], F32, name="red")
-        red_col = pool.tile([PART, 4], F32, name="red_col")
-        nc.vector.tensor_reduce(
-            out=red[:], in_=c_bank[:].rearrange("p (t n) -> p t n", t=4), axis=mybir.AxisListType.X, op=ALU.add
-        )
-        quantize_chunk(0, 1)
-        nc.vector.tensor_scalar(out=red_col[:], in0=red[:], scalar1=col_b[:, 0:1], scalar2=None, op0=ALU.mult)
         dw_out(8, scopy)
         dw_out(9, scopy)
         dw_out(10, vcopy)
@@ -411,21 +420,27 @@ def tile_capsuleneuralnetwork_pa_v_kernel(
                 dw_pass(i, g)
             if i < 2:
                 dp_index(14 + i)
-        interleave(3, 1, scopy)
-        quantize_chunk(1, 1)
         interleave(2, 1, vcopy)
+        interleave(3, 1, scopy)
+        red = pool.tile([PART, 4], F32, name="red")
+        red_col = pool.tile([PART, 4], F32, name="red_col")
+        nc.vector.tensor_reduce(
+            out=red[:], in_=c_bank[:].rearrange("p (t n) -> p t n", t=4), axis=mybir.AxisListType.X, op=ALU.add
+        )
+        quantize_chunk(1, 1)
+        nc.vector.tensor_scalar(out=red_col[:], in0=red[:], scalar1=col_b[:, 0:1], scalar2=None, op0=ALU.mult)
         last_bank = bank("c")
         for t in range(4):
             nc.tensor.transpose(
                 last_bank[:, 128 * t : 128 * (t + 1)], red_col[:, t : t + 1].to_broadcast([PART, PART]), ident[:]
             )
-        dw_out(0, vcopy)
         quantize_chunk(2, 1)
-        dw_out(1, vcopy)
-        row = pool.tile([1, G], F32, name="row")
+        dw_out(0, vcopy)
         quantize_chunk(3, 1)
-        dw_out(2, scopy)
+        dw_out(1, scopy)
+        dw_out(2, vcopy)
         dw_out(3, scopy)
+        row = pool.tile([1, G], F32, name="row")
         scopy(out=row[:].rearrange("p (m t) -> p m t", t=4), in_=last_bank[0:1, :].rearrange("p (t m) -> p m t", t=4))
         nc.sync.dma_start(out=out_1[C_OUT : C_OUT + 1, :], in_=row[:])
         for g in range(4):

from contextlib import ExitStack

import concourse.mybir as mybir
from concourse.masks import make_identity

B, T, P_IN, F, G = 256, 8, 1024, 512, 512
N = B * T
C_OUT = P_IN + F
FLOPS = 2 * N * F * G + 2 * N * G * P_IN + 2 * N * C_OUT * G
BYTES = 2 * (N * P_IN + N * F + 1 + P_IN * G + G * F + N * F) + 4 * (N * G + N * F) + 4 * (N * P_IN + (C_OUT + 1) * G)

F32 = mybir.dt.float32
BF16 = mybir.dt.bfloat16
U32 = mybir.dt.uint32
U8 = mybir.dt.uint8
E4 = mybir.dt.float8_e4m3fn_x4
E5 = mybir.dt.float8_e5m2_x4
ALU = mybir.AluOpType

PART = 128
PACK = 4
GROUP = PART * PACK
GROUPS = N // GROUP
ROLL = 128
W = (8, 8, 3, 2, 1, 1, 1, 2)


def tile_capsuleneuralnetwork_pa_v_kernel(
    tc, primary_input, prev, col, W0, b0, W1, b1, a, y, grad_out, out_0, out_1
):
    nc = tc.nc

    p_dram = primary_input.rearrange("b (t w) -> (b t) w", t=T).rearrange("(g p j) w -> g p j w", p=PART, j=PACK)
    x_dram = prev.rearrange("b (t w) -> (b t) w", t=T).rearrange("(g p j) w -> g p j w", p=PART, j=PACK)
    a_dram = a.rearrange("b t w -> (b t) w").rearrange("(g p j) w -> g p j w", p=PART, j=PACK)
    y_dram = y.rearrange("b t w -> (b t) w").rearrange("(g p j) w -> g p j w", p=PART, j=PACK)
    o_dram = out_0.rearrange("b (t w) -> (b t) w", t=T).rearrange("(g p j) w -> g p j w", p=PART, j=PACK)
    gr_rows = grad_out.rearrange("b (h w) -> (b h) w", h=2)
    gr_half = grad_out.rearrange("(g b) (h w) -> h b g w", b=PART // 2, h=2)

    with ExitStack() as ctx:
        pool = ctx.enter_context(tc.tile_pool(name="pool", bufs=1))
        psum = ctx.enter_context(tc.psum_pool(name="psum", bufs=1))

        def bank(tag):
            return psum.tile([PART, 512], F32, name=tag, tag=tag, bufs={"tp": 2, "dh": 3, "acc": 2, "c": 1}[tag])

        ident = pool.tile([PART, PART], F32, name="ident")
        swap = pool.tile([PART, PART], F32, name="swap")
        make_identity(nc, ident[:])
        for h in range(2):
            nc.gpsimd.tensor_copy(
                out=swap[:].rearrange("p (b h) -> p b h", h=2)[:, :, h],
                in_=ident[:].rearrange("p (b h) -> p b h", h=2)[:, :, 1 - h],
            )
        col_b = pool.tile([PART, 1], BF16, name="col_b")
        nc.gpsimd.dma_start(out=col_b[:], in_=col.partition_broadcast(PART))

        q_all = pool.tile([PART, GROUPS, 4 * F], BF16, name="q_all")
        w1_codes = pool.tile([PART, G], U32, name="w1_codes", align_bytes=64)
        w1_scales = pool.tile([PART, G], U8, name="w1_scales", align_bytes=64)
        w0_codes = pool.tile([PART, P_IN], U32, name="w0_codes", align_bytes=64)
        w0_scales = pool.tile([PART, P_IN], U8, name="w0_scales", align_bytes=64)

        ctx.enter_context(tc.manual_schedule())

        y_t, a_t, p_t, x_t = {}, {}, {}, {}

        def load_y(g):
            y_t[g] = pool.tile([PART, PACK, F], F32, name="y_sb", tag="y_sb", bufs=2)
            pieces = ((0, 2), (2, 4)) if g == 0 else ((0, 4),)
            nc.sync.dma_start(out=q_all[:, g, 0 : 4 * F - ROLL], in_=gr_rows[g * PART : (g + 1) * PART, ROLL : 4 * F])
            for lo, hi in pieces:
                nc.sync.dma_start(out=y_t[g][:, lo:hi, :], in_=y_dram[g][:, lo:hi, :])

        def load_a(g):
            a_t[g] = pool.tile([PART, PACK, G], F32, name="a_sb", tag="a_sb", bufs=2)
            nc.sync.dma_start(out=a_t[g][:], in_=a_dram[g])

        def load_p(g):
            p_t[g] = pool.tile([PART, PACK, P_IN], BF16, name="p_sb", tag="p_sb", bufs=4)
            nc.sync.dma_start(out=p_t[g][:], in_=p_dram[g])

        def load_x(g):
            x_t[g] = pool.tile([PART, PACK, F], BF16, name="x_sb", tag="x_sb", bufs=3)
            nc.sync.dma_start(out=x_t[g][:], in_=x_dram[g])

        def transpose_pair(words, grouped, first, engine):
            tp = bank("tp")
            for i in range(2):
                for u in range(2):
                    nc.tensor.transpose(tp[:, (2 * i + u) * 128 : (2 * i + u + 1) * 128], words(i, u), ident[:])
            dst = grouped.rearrange("p n k -> p (n k)").bitcast(F32)[:, 2 * first : 2 * first + 512]
            engine(
                out=dst.rearrange("p (t r u) -> p t r u", t=2, u=2),
                in_=tp[:].rearrange("p (t u r) -> p t r u", t=2, u=2),
            )

        load_x(0)
        w1_raw = pool.tile([PART, PACK, F], BF16, name="w1_raw", tag="x_sb", bufs=3)
        nc.sync.dma_start(out=w1_raw[:], in_=W1[0:G, :].rearrange("(m t) k -> m t k", t=PACK))
        for h in range(2):
            nc.scalar.dma_start(out=q_all[h:PART:2, :, 4 * F - ROLL : 4 * F], in_=gr_half[1 - h][:, :, 0:ROLL])
        load_x(1)
        load_y(0)
        load_p(0)
        load_a(0)
        w0_raw = pool.tile([PART, 2, PACK, G], BF16, name="w0_raw", tag="p_sb", bufs=4)
        nc.sync.dma_start(out=w0_raw[:], in_=W0[0:P_IN, :].rearrange("(n m t) k -> m n t k", n=2, t=PACK))
        load_y(1)
        load_a(1)

        def stage_tile():
            return pool.tile([PART, 512, PACK], BF16, name="stage", tag="stage", bufs=4, align_bytes=64)

        ic, isc, staged = {}, {}, {}

        def interleave(g, c, copy):
            src = x_t[g][:] if c == 2 else p_t[g][:, :, 512 * c : 512 * (c + 1)]
            staged[g, c] = stage_tile()
            copy(
                out=staged[g, c][:].rearrange("p (c i) t -> p c t i", i=4),
                in_=src.rearrange("p t (c i) -> p c t i", i=4),
            )

        def quantize_chunk(g, c):
            ic[g, c] = pool.tile([PART, 512], U32, name="ic", tag="ic", bufs=12, align_bytes=64)
            isc[g, c] = pool.tile([PART, 512], U8, name="isc", tag="isc", bufs=12, align_bytes=64)
            nc.vector.quantize_mx(
                out=ic[g, c][:].bitcast(E4), scales=isc[g, c][:], in_=staged[g, c][:].rearrange("p n k -> p (n k)")
            )

        vcopy, scopy = nc.vector.tensor_copy, nc.scalar.copy
        ac, asc, dgc, dgs, dyg, dyc, dys, dh, da, dag = ({} for i in range(10))
        c_bank = bank("c")

        ob_t = {}

        def dp_tile(g, j, engines):
            if j % 2 == 0:
                ob_t[0] = pool.tile([PART, 2, P_IN], F32, name="ob", tag="ob", bufs=4)
            ob = ob_t[0][:, j % 2, :]
            for n in range(2):
                acc = bank("acc")
                nc.tensor.matmul_mx(
                    out=acc[:],
                    lhsT=dgc[g][:, 128 * j : 128 * (j + 1)].bitcast(E5),
                    lhsT_scale=dgs[g][:, 128 * j : 128 * (j + 1)],
                    rhs=w0_codes[:, 512 * n : 512 * (n + 1)].bitcast(E4),
                    rhs_scale=w0_scales[:, 512 * n : 512 * (n + 1)],
                    start=True,
                    stop=True,
                )
                engines[n](
                    out=ob[:, 512 * n : 512 * (n + 1)].rearrange("p (m t) -> p m t", t=4),
                    in_=acc[:].rearrange("p (t m) -> p m t", t=4),
                )
            if j % 2:
                nc.sync.dma_start(out=o_dram[g][:, j - 1 : j + 1, :], in_=ob_t[0][:])

        def warm(n):
            for k in range(n):
                spare = bank("acc")
                nc.tensor.matmul(out=spare[:, 0:PART], lhsT=ident[:], rhs=ident[:], start=True, stop=True)

        def dy_half(g, i):
            if i == 0:
                dyg[g, 0] = pool.tile([PART, PACK * F], BF16, name="dy", tag="dy", bufs=1)
            cols = slice(1024 * i, 1024 * (i + 1))
            nc.vector.scalar_tensor_tensor(
                out=dyg[g, 0][:, cols],
                in0=y_t[g][:].rearrange("p j w -> p (j w)")[:, cols],
                scalar=0.0,
                in1=q_all[:, g, cols],
                op0=ALU.is_gt,
                op1=ALU.mult,
            )

        def dy_transposes(g):
            dyg[g, 1] = pool.tile([PART, 640, PACK], BF16, name="dyg", tag="dyg", bufs=1, align_bytes=64)
            dyw = dyg[g, 0][:].bitcast(F32)

            def words(j, u):
                return dyw[:, 256 * j + u : 256 * (j + 1) : 2]

            for s in range(2):
                transpose_pair(lambda i, u: words(2 * s + i, u), dyg[g, 1][:], 256 * s, scopy)
                if g == 0 and s == 0:
                    warm(W[7])
            tp = bank("tp")
            for u in range(2):
                nc.tensor.transpose(tp[:, 128 * u : 128 * (u + 1)], words(3, u), swap[:])
            scopy(
                out=dyg[g, 1][:].rearrange("p n k -> p (n k)").bitcast(F32)[:, 1024:1280].rearrange("p (r u) -> p r u", u=2),
                in_=tp[:, 0:256].rearrange("p (u r) -> p r u", u=2),
            )

        def dy_quantize(g):
            dyc[g] = pool.tile([PART, 640], U32, name="dyc", tag="dyc", bufs=2, align_bytes=64)
            dys[g] = pool.tile([PART, 640], U8, name="dys", tag="dys", bufs=2, align_bytes=64)
            for lo, hi in ((0, 512), (512, 640)):
                nc.vector.quantize_mx(
                    out=dyc[g][:, lo:hi].bitcast(E5),
                    scales=dys[g][:, lo:hi],
                    in_=dyg[g, 1][:, lo:hi, :].rearrange("p n k -> p (n k)"),
                )

        def dh_tile(g, s):
            dh[g, s] = bank("dh")
            nc.tensor.matmul_mx(
                out=dh[g, s][:],
                lhsT=dyc[g][:, 128 * s : 128 * (s + 1)].bitcast(E5),
                lhsT_scale=dys[g][:, 128 * s : 128 * (s + 1)],
                rhs=w1_codes[:].bitcast(E4),
                rhs_scale=w1_scales[:],
                start=True,
                stop=True,
            )

        def mask(g, j, s, lo, hi, src):
            nc.vector.scalar_tensor_tensor(
                out=da[g][:, j, :].rearrange("p (t m) -> p t m", t=4)[:, :, lo:hi],
                in0=a_t[g][:, j, :].rearrange("p (m t) -> p t m", t=4)[:, :, lo:hi],
                scalar=0.0,
                in1=dh[g, s][:].rearrange("p (t m) -> p t m", t=4)[:, :, src : src + hi - lo],
                op0=ALU.is_gt,
                op1=ALU.mult,
            )

        def da_transposes(g, j):
            if j == 0:
                dag[g] = pool.tile([PART, GROUP, PACK], BF16, name="dag", tag="dag", bufs=1, align_bytes=64)
            tp = bank("tp")
            for t in range(4):
                nc.tensor.transpose(tp[:, 128 * t : 128 * (t + 1)], da[g][:, j, 128 * t : 128 * (t + 1)], ident[:])
            for t in range(4):
                nc.tensor.matmul(
                    out=c_bank[:, 128 * t : 128 * (t + 1)],
                    lhsT=da[g][:, j, 128 * t : 128 * (t + 1)],
                    rhs=ident[:],
                    is_transpose=True,
                    start=(g == 0 and j == 0 and t == 0),
                    stop=(g == 3 and j == 3 and t == 3),
                )
            scopy(out=dag[g][:, 128 * j : 128 * (j + 1), :], in_=tp[:].rearrange("p (t n) -> p n t", t=4))

        interleave(0, 2, vcopy)
        load_x(2)
        w1_g = stage_tile()
        warm(W[0])
        w1_words = w1_raw[:].rearrange("p t k -> p (t k)").bitcast(F32)
        for s in range(2):
            transpose_pair(
                lambda i, u: w1_words[:, 256 * (2 * s + i) + u : 256 * (2 * s + i + 1) : 2], w1_g[:], 256 * s, scopy
            )
        warm(W[1])
        quantize_chunk(0, 2)
        nc.vector.quantize_mx(
            out=w1_codes[:].bitcast(E4), scales=w1_scales[:], in_=w1_g[:].rearrange("p n k -> p (n k)")
        )
        interleave(1, 2, vcopy)
        dy_half(0, 0)
        dy_half(0, 1)
        dy_transposes(0)
        warm(W[2])
        load_y(2)
        quantize_chunk(1, 2)
        interleave(0, 0, vcopy)
        dy_quantize(0)
        interleave(0, 1, vcopy)
        for s in (4, 0, 1):
            dh_tile(0, s)

        w0_g = {}
        w0_words = w0_raw[:].rearrange("p n t k -> p (n t k)").bitcast(F32)

        def w0_transposes(s):
            if s % 2 == 0:
                w0_g[s // 2] = stage_tile()
            transpose_pair(
                lambda i, u: w0_words[:, 256 * (2 * s + i) + u : 256 * (2 * s + i + 1) : 2],
                w0_g[s // 2][:], 256 * (s % 2), scopy,
            )

        def w0_quantize(n):
            nc.vector.quantize_mx(
                out=w0_codes[:, 512 * n : 512 * (n + 1)].bitcast(E4),
                scales=w0_scales[:, 512 * n : 512 * (n + 1)],
                in_=w0_g[n][:].rearrange("p n k -> p (n k)"),
            )

        def dp_index(k):
            if k >= 0:
                dp_tile(k // 4, k % 4, (scopy, scopy))

        at = {}

        def da_cast(g):
            at[0] = pool.tile([PART, G, PACK], BF16, name="at", tag="at", bufs=1, align_bytes=64)
            vcopy(
                out=at[0][:].rearrange("p (c i) j -> p c j i", i=4),
                in_=da[g][:].rearrange("p j (c i) -> p c j i", i=4),
            )

        def da_quantize(g):
            ac[g] = pool.tile([PART, G], U32, name="ac", tag="ac", bufs=GROUPS, align_bytes=64)
            asc[g] = pool.tile([PART, G], U8, name="asc", tag="asc", bufs=GROUPS, align_bytes=64)
            dgc[g] = pool.tile([PART, GROUP], U32, name="dgc", tag="dgc", bufs=2, align_bytes=64)
            dgs[g] = pool.tile([PART, GROUP], U8, name="dgs", tag="dgs", bufs=2, align_bytes=64)
            nc.vector.quantize_mx(out=dgc[g][:].bitcast(E5), scales=dgs[g][:], in_=dag[g][:].rearrange("p n k -> p (n k)"))
            nc.vector.quantize_mx(out=ac[g][:].bitcast(E5), scales=asc[g][:], in_=at[0][:].rearrange("p n k -> p (n k)"))

        for g in range(GROUPS):
            da[g] = pool.tile([PART, PACK, G], F32, name="da", tag="da", bufs=1)
            mask(g, 0, 4, 0, 32, 96)
            mask(g, 0, 0, 32, 128, 0)
            dh_tile(g, 2)
            mask(g, 1, 0, 0, 32, 96)
            mask(g, 1, 1, 32, 128, 0)
            dh_tile(g, 3)
            mask(g, 2, 1, 0, 32, 96)
            mask(g, 2, 2, 32, 128, 0)
            mask(g, 3, 2, 0, 32, 96)
            mask(g, 3, 3, 32, 128, 0)
            da_transposes(g, 0)
            da_transposes(g, 1)
            if g == 0:
                warm(W[3])
            dp_index(4 * g - 2)
            da_transposes(g, 2)
            da_transposes(g, 3)
            if g == 0:
                warm(W[4])
            dp_index(4 * g - 1)
            if g == 0:
                load_a(2)
                load_x(3)
                for s in range(4):
                    w0_transposes(s)
                    warm(W[5])
                da_cast(0)
                quantize_chunk(0, 0)
                quantize_chunk(0, 1)
                da_quantize(0)
            if g == 1:
                load_a(3)
                load_p(1)
            if g == 2:
                load_p(2)
                load_p(3)
            if g < 3:
                dy_half(g + 1, 0)
                dy_half(g + 1, 1)
                dy_transposes(g + 1)
            if g == 0:
                load_y(3)
                warm(W[6])
                w0_quantize(0)
                w0_quantize(1)
            else:
                da_cast(g)
                if g == 2:
                    quantize_chunk(2, 2)
                if g == 3:
                    quantize_chunk(3, 2)
                    interleave(1, 0, vcopy)
                da_quantize(g)
            if g < 3:
                dp_index(4 * g)
                dy_quantize(g + 1)
                if g > 0:
                    interleave(g + 1, 2, vcopy)
                for s in (4, 0, 1):
                    dh_tile(g + 1, s)
                dp_index(4 * g + 1)

        seq = ["tp", "dh", "dh", "dh", "tp", "tp", "acc", "acc", "dh", "dh", "dh", "tp"]
        dw_bank = {}

        def dw_pass(i, g):
            c, r = divmod(i, 4)
            if g == 0:
                dw_bank[i] = bank(seq[i])
            nc.tensor.matmul_mx(
                out=dw_bank[i][:],
                lhsT=ic[g, c][:, 128 * r : 128 * (r + 1)].bitcast(E4),
                lhsT_scale=isc[g, c][:, 128 * r : 128 * (r + 1)],
                rhs=ac[g][:].bitcast(E5),
                rhs_scale=asc[g][:],
                start=(g == 0),
                stop=(g == GROUPS - 1),
            )

        def dw_out(i, copy):
            if i % 4 == 0:
                ob_t[1] = pool.tile([PART, 4, G], F32, name="wb", tag="ob", bufs=4)
            wb = ob_t[1][:, i % 4, :]
            copy(out=wb.rearrange("p (m t) -> p m t", t=4), in_=dw_bank[i][:].rearrange("p (t m) -> p m t", t=4))
            nc.sync.dma_start(out=out_1[128 * i : 128 * (i + 1), :], in_=wb)

        interleave(3, 0, scopy)
        for i in range(8, 12):
            for g in range(3):
                dw_pass(i, g)
        interleave(2, 0, vcopy)
        quantize_chunk(1, 0)
        dp_index(12)
        for i in range(8, 12):
            dw_pass(i, 3)
        dp_index(13)
        interleave(1, 1, vcopy)
        quantize_chunk(2, 0)
        quantize_chunk(3, 0)
        dw_out(8, scopy)
        dw_out(9, scopy)
        dw_out(10, vcopy)
        dw_out(11, vcopy)
        for i in range(4):
            for g in range(4):
                dw_pass(i, g)
            if i < 2:
                dp_index(14 + i)
        interleave(2, 1, vcopy)
        interleave(3, 1, scopy)
        red = pool.tile([PART, 4], F32, name="red")
        red_col = pool.tile([PART, 4], F32, name="red_col")
        nc.vector.tensor_reduce(
            out=red[:], in_=c_bank[:].rearrange("p (t n) -> p t n", t=4), axis=mybir.AxisListType.X, op=ALU.add
        )
        quantize_chunk(1, 1)
        nc.vector.tensor_scalar(out=red_col[:], in0=red[:], scalar1=col_b[:, 0:1], scalar2=None, op0=ALU.mult)
        last_bank = bank("c")
        for t in range(4):
            nc.tensor.transpose(
                last_bank[:, 128 * t : 128 * (t + 1)], red_col[:, t : t + 1].to_broadcast([PART, PART]), ident[:]
            )
        quantize_chunk(2, 1)
        dw_out(0, vcopy)
        quantize_chunk(3, 1)
        dw_out(1, scopy)
        dw_out(2, vcopy)
        dw_out(3, scopy)
        row = pool.tile([1, G], F32, name="row")
        scopy(out=row[:].rearrange("p (m t) -> p m t", t=4), in_=last_bank[0:1, :].rearrange("p (t m) -> p m t", t=4))
        nc.sync.dma_start(out=out_1[C_OUT : C_OUT + 1, :], in_=row[:])
        for g in range(4):
            for i in range(4, 8):
                dw_pass(i, g)
        for i in range(4, 8):
            dw_out(i, scopy if i % 2 == 0 else vcopy)
